import numpy as np
import ml_dtypes


def mxq(x, axis, fmt="e4m3"):
    dtype, down = {"e4m3": (ml_dtypes.float8_e4m3fn, 7), "e5m2": (ml_dtypes.float8_e5m2, 14)}[fmt]
    v = np.moveaxis(np.asarray(x, np.float32).astype(ml_dtypes.bfloat16).astype(np.float64), axis, -1)
    blocks = v.reshape(v.shape[:-1] + (-1, 32))
    amax = np.abs(blocks).max(-1, keepdims=True)
    byte = np.maximum(np.where(amax > 0, np.frexp(amax)[1] - 1 + 127, 0) - down, 1)
    scale = np.exp2(byte - 127.0)
    codes = (blocks / scale).astype(np.float32).astype(dtype).astype(np.float64)
    return np.moveaxis((codes * scale).reshape(v.shape), -1, axis)


WIDE = False


def mx_kscale(k):
    if not WIDE:
        return np.ones(k)
    levels = np.array([10, -10, 5, -5, 0])
    if k % 512:
        return np.exp2(np.random.permutation(np.resize(levels, k // 32))).repeat(32)
    a = np.empty((k // 512, 16))
    for p in range(k // 512):
        a[p, :8] = np.random.permutation(np.resize(levels, 8))
        for g in range(8):
            far = levels[np.abs(levels - a[p, g]) >= 10]
            a[p, g + 8] = far[np.random.randint(len(far))]
    return np.exp2(a.ravel()).repeat(32)


BF16 = ml_dtypes.bfloat16


def bf(x):
    return np.asarray(x, np.float32).astype(BF16)


def f64(x):
    return np.asarray(x).astype(np.float64)


B, S, H, HD = 8, 512, 512, 128
NH = H // HD
HALF = HD // 2
WS = 1.5 * (HD / H) ** 0.25 / np.sqrt(H)


def rotate_half(u):
    return np.concatenate((-u[..., HALF:], u[..., :HALF]), axis=-1)


def rope(u, c, s):
    u4 = u.reshape(B, S, NH, HD)
    return (u4 * c[None, :, None, :] + rotate_half(u4) * s[None, :, None, :]).reshape(B, S, H)


def setup_inputs():
    s = mx_kscale(H)
    t = np.tile(mx_kscale(H).reshape(NH, 2, HALF)[:, :1, :], (1, 2, 1)).reshape(H)
    return {"hidden_states": bf(np.random.standard_normal((B, S, H)) * s),
            "wq_deq": bf(np.random.standard_normal((H, H)) * WS * t[:, None] / s[None, :]),
            "wk_deq": bf(np.random.standard_normal((H, H)) * WS / t[:, None] / s[None, :]),
            "cos": bf(np.random.random((S, HD))),
            "sin": bf(np.random.random((S, HD))),
            "attention_mask": bf(np.random.standard_normal((1, S, S)) * 0.5)}


def reference(hidden_states, wq_deq, wk_deq, cos, sin, attention_mask):
    xq = mxq(f64(hidden_states), 2, "e4m3")
    q = xq @ mxq(f64(wq_deq), 1, "e4m3").T
    k = xq @ mxq(f64(wk_deq), 1, "e4m3").T
    q_rot = rope(q, f64(cos), f64(sin))
    k_rot = rope(k, f64(cos), f64(sin))
    scores = (mxq(q_rot, 2, "e4m3") @ mxq(k_rot, 2, "e4m3").transpose(0, 2, 1)) / np.sqrt(HD)
    return scores + f64(attention_mask)

@@ -1,0 +1,215 @@
+from contextlib import ExitStack
+import math
+
+import concourse.mybir as mybir
+from concourse.masks import make_identity
+
+F32 = mybir.dt.float32
+BF16 = mybir.dt.bfloat16
+U32 = mybir.dt.uint32
+U8 = mybir.dt.uint8
+FP8X4 = mybir.dt.float8_e4m3fn_x4
+MULT = mybir.AluOpType.mult
+ADD = mybir.AluOpType.add
+
+P = 128
+B, S, H, HD = 8, 512, 512, 128
+CHUNKS = H // HD
+PACK = 4
+RUN = HD // PACK
+HALF_RUN = RUN // 2
+TILES = S // P
+UNITS = B * TILES
+SCORE_LAG = TILES + 1
+INV_SQRT_HD = 1.0 / math.sqrt(HD)
+
+FLOPS = 2 * (2 * B * S * H * H) + 2 * B * S * S * H
+
+
+def tile_llamaattention_pa_t_kernel(
+    tc, hidden_states, wq_deq, wk_deq, cos, sin, attention_mask, out
+):
+    nc = tc.nc
+    with ExitStack() as ctx:
+        keep = ctx.enter_context(tc.tile_pool(name="keep", bufs=1))
+        stage = ctx.enter_context(tc.tile_pool(name="stage", bufs=2))
+        products = ctx.enter_context(tc.tile_pool(name="products", bufs=3))
+        results = ctx.enter_context(tc.tile_pool(name="results", bufs=4))
+        psum = ctx.enter_context(tc.psum_pool(name="psum", bufs=1))
+        ctx.enter_context(tc.manual_schedule())
+
+        wq_rows = keep.tile([P, TILES, H], BF16)
+        wk_rows = keep.tile([P, TILES, H], BF16)
+        x_rows = [keep.tile([P, TILES, H], BF16, name="x_rows%d" % b) for b in range(B)]
+        cos_rows = keep.tile([P, TILES, HD], BF16)
+        sin_rows = keep.tile([P, TILES, HD], BF16)
+        cos_table = keep.tile([P, TILES, PACK, RUN], BF16)
+        sin_table = keep.tile([P, TILES, PACK, RUN], BF16)
+        mask_rows = keep.tile([P, TILES, S], BF16)
+
+        def load_x(b):
+            nc.sync.dma_start(
+                out=x_rows[b][:],
+                in_=hidden_states[b].rearrange("(t p) k -> p t k", p=P),
+            )
+
+        nc.sync.dma_start(out=wq_rows[:], in_=wq_deq.rearrange("(p t) k -> p t k", p=P))
+        nc.sync.dma_start(out=wk_rows[:], in_=wk_deq.rearrange("(p t) k -> p t k", p=P))
+        load_x(0)
+        nc.sync.dma_start(out=cos_rows[:], in_=cos.rearrange("(t p) f -> p t f", p=P))
+        nc.sync.dma_start(out=sin_rows[:], in_=sin.rearrange("(t p) f -> p t f", p=P))
+        load_x(1)
+        nc.sync.dma_start(out=mask_rows[:], in_=attention_mask[0].rearrange("(t p) k -> p t k", p=P))
+        for b in range(2, B):
+            load_x(b)
+
+        identity = keep.tile([P, P], F32)
+        make_identity(nc, identity[:])
+
+        cos_by_code = cos_rows[:].rearrange("p s (f q) -> p s q f", q=PACK)
+        sin_by_code = sin_rows[:].rearrange("p s (f q) -> p s q f", q=PACK)
+        for table, rows, part, sign in (
+            (cos_table, cos_by_code, slice(0, RUN), 1.0),
+            (sin_table, sin_by_code, slice(0, HALF_RUN), -1.0),
+            (sin_table, sin_by_code, slice(HALF_RUN, RUN), 1.0),
+        ):
+            nc.gpsimd.tensor_scalar(
+                out=table[:, :, :, part], in0=rows[:, :, :, part], scalar1=sign, scalar2=0.0, op0=MULT, op1=ADD
+            )
+
+        def turn_two_tiles(words, grouped_words, copy_out):
+            bank = psum.tile([P, 2, 2, P], F32, tag="turn_or_scores", bufs=2)
+            for r in range(2):
+                for u in range(2):
+                    nc.tensor.transpose(bank[:, r, u, :], words[:, r, u : 2 * P : 2], identity[:])
+            copy_out(
+                out=grouped_words.rearrange("p (r n) u -> p r n u", r=2),
+                in_=bank[:].rearrange("p r u n -> p r n u"),
+            )
+
+        def quantise(pool, grouped, tag):
+            codes = pool.tile([P, 512], U32, tag=tag + "_codes", align_bytes=64)
+            scales = pool.tile([P, 512], U8, tag=tag + "_scales", align_bytes=64)
+            nc.vector.quantize_mx(
+                out=codes[:].bitcast(FP8X4),
+                scales=scales[:],
+                in_=grouped[:].rearrange("p n t -> p (n t)"),
+            )
+            return codes, scales
+
+        def mx_pass(acc, stationary, t, moving):
+            cols = slice(t * P, (t + 1) * P)
+            nc.tensor.matmul_mx(
+                out=acc,
+                lhsT=stationary[0][:, cols].bitcast(FP8X4),
+                lhsT_scale=stationary[1][:, cols],
+                rhs=moving[0][:].bitcast(FP8X4),
+                rhs_scale=moving[1][:],
+                start=True,
+                stop=True,
+            )
+
+        w_mx = {}
+        x_grouped = {}
+        x_mx = {}
+        raw = {}
+        rot_grouped = {}
+        rot_mx = {}
+
+        def turn_x(b, half):
+            if half == 0:
+                x_grouped[b] = stage.tile([P, S, PACK], BF16, name="x_grouped", tag="x_grouped", align_bytes=64)
+            first = 2 * half
+            turn_two_tiles(
+                x_rows[b][:].bitcast(F32)[:, first : first + 2, :],
+                x_grouped[b][:].bitcast(F32)[:, first * P : (first + 2) * P, :],
+                nc.scalar.copy,
+            )
+
+        def project(i):
+            b, t = divmod(i, TILES)
+            for name in ("q", "k"):
+                raw[name, i] = psum.tile([P, H], F32, name=name + "_raw", tag=name + "_raw", bufs=2)
+                mx_pass(raw[name, i][:], x_mx[b], t, w_mx[name])
+
+        def rope(name, i):
+            b, t = divmod(i, TILES)
+            low, high = slice(0, HALF_RUN), slice(HALF_RUN, RUN)
+            u = raw[name, i][:].rearrange("p (q c f) -> p q c f", q=PACK, c=CHUNKS)
+            straight = products.tile([P, PACK, CHUNKS, RUN], F32)
+            crossed = products.tile([P, PACK, CHUNKS, RUN], F32)
+
+            def factor(table, part):
+                f = table[:, t, :, part]
+                return f.unsqueeze(2).to_broadcast([P, PACK, CHUNKS, f.shape[2]])
+
+            nc.vector.tensor_tensor(out=straight[:], in0=u, in1=factor(cos_table, slice(0, RUN)), op=MULT)
+            nc.vector.tensor_tensor(
+                out=crossed[:, :, :, low], in0=u[:, :, :, high], in1=factor(sin_table, low), op=MULT
+            )
+            nc.vector.tensor_tensor(
+                out=crossed[:, :, :, high], in0=u[:, :, :, low], in1=factor(sin_table, high), op=MULT
+            )
+            turned = psum.tile([P, PACK, P], F32, tag=name + "_turned")
+            for c in range(PACK):
+                nc.tensor.matmul(
+                    out=turned[:, c, :], lhsT=straight[:, c].rearrange("p c f -> p (c f)"), rhs=identity[:],
+                    is_transpose=True, start=True, stop=False,
+                )
+                nc.tensor.matmul(
+                    out=turned[:, c, :], lhsT=crossed[:, c].rearrange("p c f -> p (c f)"), rhs=identity[:],
+                    is_transpose=True, start=False, stop=True,
+                )
+            if t == 0:
+                rot_grouped[name, b] = stage.tile(
+                    [P, S, PACK], BF16, name=name + "_rot", tag=name + "_rot", align_bytes=64
+                )
+            nc.scalar.copy(
+                out=rot_grouped[name, b][:, t * P : (t + 1) * P, :],
+                in_=turned[:].rearrange("p c n -> p n c"),
+            )
+
+        def score_pass(j):
+            b, t = divmod(j, TILES)
+            scores = psum.tile([P, S], F32, tag="turn_or_scores", bufs=2)
+            mx_pass(scores[:], rot_mx["q", b], t, rot_mx["k", b])
+            return scores
+
+        def finish(j, scores):
+            b, t = divmod(j, TILES)
+            result = results.tile([P, S], F32)
+            nc.scalar.mul(out=result[:], in_=scores[:], mul=INV_SQRT_HD)
+            nc.gpsimd.tensor_tensor(out=result[:], in0=result[:], in1=mask_rows[:, t, :], op=ADD)
+            nc.sync.dma_start(out=out[b, t * P : (t + 1) * P, :], in_=result[:])
+
+        for name, rows in (("q", wq_rows), ("k", wk_rows)):
+            w_grouped = keep.tile([P, H, PACK], BF16, tag=name + "_w_grouped", align_bytes=64)
+            for first in (0, 2):
+                turn_two_tiles(
+                    rows[:].bitcast(F32)[:, first : first + 2, :],
+                    w_grouped[:].bitcast(F32)[:, first * P : (first + 2) * P, :],
+                    nc.vector.tensor_copy,
+                )
+            w_mx[name] = quantise(keep, w_grouped, name + "_w")
+        turn_x(0, 0)
+        turn_x(0, 1)
+        x_mx[0] = quantise(stage, x_grouped[0], "x")
+        project(0)
+
+        for i in range(UNITS + SCORE_LAG):
+            b, t = divmod(i, TILES)
+            j = i - SCORE_LAG
+            if i + 1 < UNITS:
+                project(i + 1)
+            if j >= 0:
+                finish(j, score_pass(j))
+            if t < 2 and b + 1 < B:
+                turn_x(b + 1, t)
+            if i < UNITS:
+                rope("q", i)
+                rope("k", i)
+            if t == 0 and 1 <= b <= B:
+                rot_mx["q", b - 1] = quantise(stage, rot_grouped["q", b - 1], "q_rot")
+                rot_mx["k", b - 1] = quantise(stage, rot_grouped["k", b - 1], "k_rot")
+            if t == 2 and b + 1 < B:
+                x_mx[b + 1] = quantise(stage, x_grouped[b + 1], "x")

@@ -1,9 +1,7 @@
 from contextlib import ExitStack
 import math
-
 import concourse.mybir as mybir
 from concourse.masks import make_identity
-
 F32 = mybir.dt.float32
 BF16 = mybir.dt.bfloat16
 U32 = mybir.dt.uint32
@@ -11,7 +9,6 @@ U8 = mybir.dt.uint8
 FP8X4 = mybir.dt.float8_e4m3fn_x4
 MULT = mybir.AluOpType.mult
 ADD = mybir.AluOpType.add
-
 P = 128
 B, S, H, HD = 8, 512, 512, 128
 CHUNKS = H // HD
@@ -19,197 +16,237 @@ PACK = 4
 RUN = HD // PACK
 HALF_RUN = RUN // 2
 TILES = S // P
-UNITS = B * TILES
-SCORE_LAG = TILES + 1
 INV_SQRT_HD = 1.0 / math.sqrt(HD)
-
 FLOPS = 2 * (2 * B * S * H * H) + 2 * B * S * S * H
+PAIRS = 4 * B
+K = dict(WJ=0, XP=0, GP="low2", MASKV=0, WEVERY=0, SPLITMASK=1, LAGS=(4, 5, 6, 7), TAILV=1, QPOS=1)
 
-
-def tile_llamaattention_pa_t_kernel(
-    tc, hidden_states, wq_deq, wk_deq, cos, sin, attention_mask, out
-):
+def tile_llamaattention_pa_t_kernel(tc, hidden_states, wq_deq, wk_deq, cos, sin, attention_mask, out):
     nc = tc.nc
     with ExitStack() as ctx:
         keep = ctx.enter_context(tc.tile_pool(name="keep", bufs=1))
         stage = ctx.enter_context(tc.tile_pool(name="stage", bufs=2))
-        products = ctx.enter_context(tc.tile_pool(name="products", bufs=3))
-        results = ctx.enter_context(tc.tile_pool(name="results", bufs=4))
+        products = ctx.enter_context(tc.tile_pool(name="products", bufs=4))
+        results = ctx.enter_context(tc.tile_pool(name="results", bufs=6))
         psum = ctx.enter_context(tc.psum_pool(name="psum", bufs=1))
         ctx.enter_context(tc.manual_schedule())
-
-        wq_rows = keep.tile([P, TILES, H], BF16)
-        wk_rows = keep.tile([P, TILES, H], BF16)
+        w_rows = {n: keep.tile([P, TILES, H], BF16, name="w_rows" + n) for n in "qk"}
         x_rows = [keep.tile([P, TILES, H], BF16, name="x_rows%d" % b) for b in range(B)]
         cos_rows = keep.tile([P, TILES, HD], BF16)
         sin_rows = keep.tile([P, TILES, HD], BF16)
         cos_table = keep.tile([P, TILES, PACK, RUN], BF16)
         sin_table = keep.tile([P, TILES, PACK, RUN], BF16)
         mask_rows = keep.tile([P, TILES, S], BF16)
+        ident = keep.tile([P, P], F32)
+        make_identity(nc, ident[:])
 
-        def load_x(b):
-            nc.sync.dma_start(
-                out=x_rows[b][:],
-                in_=hidden_states[b].rearrange("(t p) k -> p t k", p=P),
-            )
-
-        nc.sync.dma_start(out=wq_rows[:], in_=wq_deq.rearrange("(p t) k -> p t k", p=P))
-        nc.sync.dma_start(out=wk_rows[:], in_=wk_deq.rearrange("(p t) k -> p t k", p=P))
-        load_x(0)
+        def load_w(n, w, h):
+            nc.sync.dma_start(out=w_rows[n][:, 2*h:2*h+2], in_=w.rearrange("(p t) k -> p t k", p=P)[:, 2*h:2*h+2])
+        def load_x(b, t0, t1):
+            nc.sync.dma_start(out=x_rows[b][:, t0:t1], in_=hidden_states[b].rearrange("(t p) k -> p t k", p=P)[:, t0:t1])
+        load_w("k", wk_deq, 0)
+        load_w("k", wk_deq, 1)
+        load_x(0, 0, 2)
+        load_x(0, 2, 4)
         nc.sync.dma_start(out=cos_rows[:], in_=cos.rearrange("(t p) f -> p t f", p=P))
         nc.sync.dma_start(out=sin_rows[:], in_=sin.rearrange("(t p) f -> p t f", p=P))
-        load_x(1)
+        load_w("q", wq_deq, 0)
+        load_w("q", wq_deq, 1)
+        load_x(1, 0, 4)
         nc.sync.dma_start(out=mask_rows[:], in_=attention_mask[0].rearrange("(t p) k -> p t k", p=P))
         for b in range(2, B):
-            load_x(b)
-
-        identity = keep.tile([P, P], F32)
-        make_identity(nc, identity[:])
-
+            load_x(b, 0, 4)
         cos_by_code = cos_rows[:].rearrange("p s (f q) -> p s q f", q=PACK)
         sin_by_code = sin_rows[:].rearrange("p s (f q) -> p s q f", q=PACK)
-        for table, rows, part, sign in (
-            (cos_table, cos_by_code, slice(0, RUN), 1.0),
-            (sin_table, sin_by_code, slice(0, HALF_RUN), -1.0),
-            (sin_table, sin_by_code, slice(HALF_RUN, RUN), 1.0),
-        ):
-            nc.gpsimd.tensor_scalar(
-                out=table[:, :, :, part], in0=rows[:, :, :, part], scalar1=sign, scalar2=0.0, op0=MULT, op1=ADD
-            )
+        def tables():
+            for table, rows, part, sign in (
+                (cos_table, cos_by_code, slice(0, RUN), 1.0),
+                (sin_table, sin_by_code, slice(0, HALF_RUN), -1.0),
+                (sin_table, sin_by_code, slice(HALF_RUN, RUN), 1.0),
+            ):
+                nc.scalar.mul(out=table[:, :, :, part], in_=rows[:, :, :, part], mul=sign)
 
-        def turn_two_tiles(words, grouped_words, copy_out):
-            bank = psum.tile([P, 2, 2, P], F32, tag="turn_or_scores", bufs=2)
+        def turn_two_tiles(words, grouped_words, copy_out, tag="misc"):
+            bank = psum.tile([P, 2, 2, P], F32, name="bank", tag=tag, bufs=4 if tag == "raw" else 2)
             for r in range(2):
                 for u in range(2):
-                    nc.tensor.transpose(bank[:, r, u, :], words[:, r, u : 2 * P : 2], identity[:])
-            copy_out(
-                out=grouped_words.rearrange("p (r n) u -> p r n u", r=2),
-                in_=bank[:].rearrange("p r u n -> p r n u"),
-            )
+                    nc.tensor.transpose(bank[:, r, u, :], words[:, r, u : 2 * P : 2] if words.ndim == 3 else words[:, r, u, :], ident[:])
+            copy_out(out=grouped_words.rearrange("p (r n) u -> p r n u", r=2), in_=bank[:].rearrange("p r u n -> p r n u"))
 
-        def quantise(pool, grouped, tag):
-            codes = pool.tile([P, 512], U32, tag=tag + "_codes", align_bytes=64)
-            scales = pool.tile([P, 512], U8, tag=tag + "_scales", align_bytes=64)
-            nc.vector.quantize_mx(
-                out=codes[:].bitcast(FP8X4),
-                scales=scales[:],
-                in_=grouped[:].rearrange("p n t -> p (n t)"),
-            )
-            return codes, scales
+        def new_mx(pool, tag):
+            return (pool.tile([P, 512], U32, name=tag + "_codes", tag=tag + "_codes", align_bytes=64), pool.tile([P, 512], U8, name=tag + "_scales", tag=tag + "_scales", align_bytes=64))
 
-        def mx_pass(acc, stationary, t, moving):
+        def quantise(mx, grouped, lo, hi):
+            nc.vector.quantize_mx(out=mx[0][:, lo:hi].bitcast(FP8X4), scales=mx[1][:, lo:hi], in_=grouped[:, lo:hi].rearrange("p n t -> p (n t)"))
+
+        def mx_pass(acc, st, t, mov):
             cols = slice(t * P, (t + 1) * P)
-            nc.tensor.matmul_mx(
-                out=acc,
-                lhsT=stationary[0][:, cols].bitcast(FP8X4),
-                lhsT_scale=stationary[1][:, cols],
-                rhs=moving[0][:].bitcast(FP8X4),
-                rhs_scale=moving[1][:],
-                start=True,
-                stop=True,
-            )
+            nc.tensor.matmul_mx(out=acc, lhsT=st[0][:, cols].bitcast(FP8X4), lhsT_scale=st[1][:, cols], rhs=mov[0][:].bitcast(FP8X4), rhs_scale=mov[1][:], start=True, stop=True)
 
-        w_mx = {}
-        x_grouped = {}
-        x_mx = {}
-        raw = {}
-        rot_grouped = {}
-        rot_mx = {}
+        w_mx, x_g, x_mx, raw, rot_g, rot_mx, prod = {}, {}, {}, {}, {}, {}, {}
 
-        def turn_x(b, half):
-            if half == 0:
-                x_grouped[b] = stage.tile([P, S, PACK], BF16, name="x_grouped", tag="x_grouped", align_bytes=64)
-            first = 2 * half
-            turn_two_tiles(
-                x_rows[b][:].bitcast(F32)[:, first : first + 2, :],
-                x_grouped[b][:].bitcast(F32)[:, first * P : (first + 2) * P, :],
-                nc.scalar.copy,
-            )
+        xp = {}
+        def permute_x(b, h):
+            xp[b, h] = stage.tile([P, 2, 2, P], F32, name="xp", tag="xp")
+            nc.scalar.copy(out=xp[b, h][:], in_=x_rows[b][:].bitcast(F32)[:, 2*h:2*h+2, :].rearrange("p r (n u) -> p r u n", u=2))
+        def turn_x(b, h, eng=None):
+            if h == 0:
+                x_g[b] = stage.tile([P, S, PACK], BF16, name="x_g", tag="x_g", align_bytes=64)
+                x_mx[b] = new_mx(stage, "x")
+            f = 2 * h
+            turn_two_tiles(xp[b, h][:] if (b, h) in xp else x_rows[b][:].bitcast(F32)[:, f : f + 2, :], x_g[b][:].rearrange("p n t -> p (n t)").bitcast(F32).rearrange("p (n u) -> p n u", u=2)[:, f * P : (f + 2) * P, :], eng or nc.scalar.copy)
+        def quant_x(b, h):
+            quantise(x_mx[b], x_g[b], h * 256, h * 256 + 256)
 
-        def project(i):
-            b, t = divmod(i, TILES)
-            for name in ("q", "k"):
-                raw[name, i] = psum.tile([P, H], F32, name=name + "_raw", tag=name + "_raw", bufs=2)
-                mx_pass(raw[name, i][:], x_mx[b], t, w_mx[name])
+        def jobs(s):
+            b, r = divmod(s, 4)
+            n = "kkqq"[r]
+            return [(n, b, 2 * (r % 2)), (n, b, 2 * (r % 2) + 1)]
+        def gparts(s, k):
+            if is_w(s, k): return []
+            if K["GP"] == "low2": return ["low"] if k == 1 else []
+            if K["GP"] == "none": return []
+            if K["GP"] == "low12": return ["low"]
+            if K["GP"] == "both2odd": return ["low", "high"] if k == 1 and s % 2 else []
+            if K["GP"] == "lowodd": return ["low"] if k == 1 and s % 2 else []
+        def is_w(s, k):
+            return K["WJ"] and k == 0 and s % K["WJ"] == K["WJ"] - 1 and s < PAIRS - 2
+        sums = {}
+        PART = dict(low=slice(0, HALF_RUN), high=slice(HALF_RUN, RUN))
+        OTHER = dict(low="high", high="low")
 
-        def rope(name, i):
-            b, t = divmod(i, TILES)
-            low, high = slice(0, HALF_RUN), slice(HALF_RUN, RUN)
-            u = raw[name, i][:].rearrange("p (q c f) -> p q c f", q=PACK, c=CHUNKS)
-            straight = products.tile([P, PACK, CHUNKS, RUN], F32)
-            crossed = products.tile([P, PACK, CHUNKS, RUN], F32)
-
-            def factor(table, part):
-                f = table[:, t, :, part]
-                return f.unsqueeze(2).to_broadcast([P, PACK, CHUNKS, f.shape[2]])
-
-            nc.vector.tensor_tensor(out=straight[:], in0=u, in1=factor(cos_table, slice(0, RUN)), op=MULT)
-            nc.vector.tensor_tensor(
-                out=crossed[:, :, :, low], in0=u[:, :, :, high], in1=factor(sin_table, low), op=MULT
-            )
-            nc.vector.tensor_tensor(
-                out=crossed[:, :, :, high], in0=u[:, :, :, low], in1=factor(sin_table, high), op=MULT
-            )
-            turned = psum.tile([P, PACK, P], F32, tag=name + "_turned")
+        def project(s):
+            for j in jobs(s):
+                raw[j] = psum.tile([P, H], F32, name="raw", tag="raw", bufs=4)
+                mx_pass(raw[j][:], x_mx[j[1]], j[2], w_mx[j[0]])
+        def view(ap): return ap.rearrange("p (q c f) -> p q c f", q=PACK, c=CHUNKS)
+        def factor(table, t, part):
+            f = table[:, t, :, part]
+            return f.unsqueeze(2).to_broadcast([P, PACK, CHUNKS, f.shape[2]])
+        def g_side(s):
+            for k, j in enumerate(jobs(s)):
+                prod[j] = (products.tile([P, PACK, CHUNKS, RUN], F32, name="straight", tag="straight"), products.tile([P, PACK, CHUNKS, RUN], F32, name="crossed", tag="crossed"))
+                for part in gparts(s, k):
+                    tmp = results.tile([P, PACK, CHUNKS, HALF_RUN], F32, name="tmp", tag="tmp")
+                    nc.scalar.copy(out=tmp[:], in_=view(raw[j][:])[:, :, :, PART[OTHER[part]]])
+                    nc.gpsimd.tensor_tensor(out=prod[j][1][:][:, :, :, PART[part]], in0=tmp[:], in1=factor(sin_table, j[2], PART[part]), op=MULT)
+        def v_side(s, k):
+            j = jobs(s)[k]
+            nc.vector.tensor_tensor(out=prod[j][0][:], in0=view(raw[j][:]), in1=factor(cos_table, j[2], slice(0, RUN)), op=MULT)
+            for part in ("low", "high"):
+                if part not in gparts(s, k):
+                    nc.vector.tensor_tensor(out=prod[j][1][:, :, :, PART[part]], in0=view(raw[j][:])[:, :, :, PART[OTHER[part]]], in1=factor(sin_table, j[2], PART[part]), op=MULT)
+            if is_w(s, k):
+                sums[j] = products.tile([P, 2, CHUNKS * RUN, 2], BF16, name="sums", tag="sums")
+                a, c = [x[:].rearrange("p (u e) c f -> p u (c f) e", u=2) for x in prod[j]]
+                for h in range(K["SPLITMASK"]):
+                    hs = slice(h * 2 // K["SPLITMASK"], (h + 1) * 2 // K["SPLITMASK"])
+                    nc.gpsimd.tensor_tensor(out=sums[j][:, hs], in0=a[:, hs], in1=c[:, hs], op=ADD)
+        turned = {}
+        def t_side(s, k):
+            n, b, t = j = jobs(s)[k]
+            tn = psum.tile([P, PACK, P], F32, name="turned", tag="turned", bufs=2)
+            if is_w(s, k):
+                for u in range(2):
+                    nc.tensor.transpose(tn[:, u, :], sums[j][:].rearrange("p u n e -> p (u n e)").bitcast(F32)[:, u * P : u * P + P], ident[:])
+                turned[j] = tn
+                return
             for c in range(PACK):
-                nc.tensor.matmul(
-                    out=turned[:, c, :], lhsT=straight[:, c].rearrange("p c f -> p (c f)"), rhs=identity[:],
-                    is_transpose=True, start=True, stop=False,
-                )
-                nc.tensor.matmul(
-                    out=turned[:, c, :], lhsT=crossed[:, c].rearrange("p c f -> p (c f)"), rhs=identity[:],
-                    is_transpose=True, start=False, stop=True,
-                )
-            if t == 0:
-                rot_grouped[name, b] = stage.tile(
-                    [P, S, PACK], BF16, name=name + "_rot", tag=name + "_rot", align_bytes=64
-                )
-            nc.scalar.copy(
-                out=rot_grouped[name, b][:, t * P : (t + 1) * P, :],
-                in_=turned[:].rearrange("p c n -> p n c"),
-            )
+                for i in (0, 1):
+                    nc.tensor.matmul(out=tn[:, c, :], lhsT=prod[j][i][:, c].rearrange("p c f -> p (c f)"), rhs=ident[:], is_transpose=True, start=i == 0, stop=i == 1)
+            turned[j] = tn
+        def s_side(s, k, eng=None):
+            n, b, t = j = jobs(s)[k]
+            if (n, b) not in rot_g:
+                rot_g[n, b] = stage.tile([P, S, PACK], BF16, name=n + "_rot", tag=n + "_rot", align_bytes=64)
+                rot_mx[n, b] = new_mx(stage, n + "rot")
+            if is_w(s, k):
+                (eng or nc.scalar.copy)(out=rot_g[n, b][:].rearrange("p n t -> p (n t)").bitcast(F32).rearrange("p (n u) -> p n u", u=2)[:, t * P : (t + 1) * P, :], in_=turned[j][:, 0:2].rearrange("p c n -> p n c"))
+                return
+            (eng or nc.scalar.copy)(out=rot_g[n, b][:, t * P : (t + 1) * P, :], in_=turned[j][:].rearrange("p c n -> p n c"))
+        def quant_rot(s):
+            n, b, t = jobs(s)[0]
+            quantise(rot_mx[n, b], rot_g[n, b], t * P, t * P + 256)
+        def score(b, t):
+            sc = psum.tile([P, S], F32, name="scores", tag="misc", bufs=2)
+            mx_pass(sc[:], rot_mx["q", b], t, rot_mx["k", b])
+            return sc
+        def finish(b, t, sc, onv=False):
+            res = results.tile([P, S], F32, name="res", tag="res")
+            if onv:
+                nc.vector.scalar_tensor_tensor(out=res[:], in0=sc[:], scalar=INV_SQRT_HD, in1=mask_rows[:, t, :], op0=MULT, op1=ADD)
+            else:
+                nc.scalar.mul(out=res[:], in_=sc[:], mul=INV_SQRT_HD)
+                w = S // K["SPLITMASK"]
+                for h in range(K["SPLITMASK"]):
+                    nc.gpsimd.tensor_tensor(out=res[:, h*w:h*w+w], in0=res[:, h*w:h*w+w], in1=mask_rows[:, t, h*w:h*w+w], op=ADD)
+            nc.sync.dma_start(out=out[b, t * P : (t + 1) * P, :], in_=res[:])
 
-        def score_pass(j):
-            b, t = divmod(j, TILES)
-            scores = psum.tile([P, S], F32, tag="turn_or_scores", bufs=2)
-            mx_pass(scores[:], rot_mx["q", b], t, rot_mx["k", b])
-            return scores
-
-        def finish(j, scores):
-            b, t = divmod(j, TILES)
-            result = results.tile([P, S], F32)
-            nc.scalar.mul(out=result[:], in_=scores[:], mul=INV_SQRT_HD)
-            nc.gpsimd.tensor_tensor(out=result[:], in0=result[:], in1=mask_rows[:, t, :], op=ADD)
-            nc.sync.dma_start(out=out[b, t * P : (t + 1) * P, :], in_=result[:])
-
-        for name, rows in (("q", wq_rows), ("k", wk_rows)):
-            w_grouped = keep.tile([P, H, PACK], BF16, tag=name + "_w_grouped", align_bytes=64)
-            for first in (0, 2):
-                turn_two_tiles(
-                    rows[:].bitcast(F32)[:, first : first + 2, :],
-                    w_grouped[:].bitcast(F32)[:, first * P : (first + 2) * P, :],
-                    nc.vector.tensor_copy,
-                )
-            w_mx[name] = quantise(keep, w_grouped, name + "_w")
-        turn_x(0, 0)
+        wg = {}
+        def turn_w(n, h, eng):
+            if h == 0:
+                wg[n] = keep.tile([P, H, PACK], BF16, name=n + "_w_g", tag=n + "_w_g", align_bytes=64)
+                w_mx[n] = new_mx(keep, n + "_w")
+            f = 2 * h
+            turn_two_tiles(w_rows[n][:].bitcast(F32)[:, f : f + 2, :], wg[n][:].rearrange("p n t -> p (n t)").bitcast(F32).rearrange("p (n u) -> p n u", u=2)[:, f * P : (f + 2) * P, :], eng, tag="raw")
+        def quant_w(n, h): quantise(w_mx[n], wg[n], 256 * h, 256 * h + 256)
+        turn_w("k", 0, nc.vector.tensor_copy)
+        turn_w("k", 1, nc.scalar.copy)
+        turn_x(0, 0, nc.vector.tensor_copy)
         turn_x(0, 1)
-        x_mx[0] = quantise(stage, x_grouped[0], "x")
+        quant_w("k", 0)
+        quant_w("k", 1)
+        quant_x(0, 0)
+        tables()
         project(0)
+        turn_w("q", 0, nc.scalar.copy)
+        turn_w("q", 1, nc.scalar.copy)
+        g_side(0)
+        pending = []
+        sched = {}
+        for b in range(B):
+            for t in range(TILES):
+                st = 4 * b + K["LAGS"][t]
+                if b == B - 1: st = 99
+                if st == 32: st = 31
+                sched.setdefault(st, []).append((b, t))
+        for s in range(PAIRS):
+            b, r = divmod(s, 4)
+            if s == 0:
+                v_side(s, 0)
+                quant_x(0, 1)
+            if s + 1 < PAIRS:
+                project(s + 1)
+            if 0 < s < PAIRS: v_side(s, 0)
 
-        for i in range(UNITS + SCORE_LAG):
-            b, t = divmod(i, TILES)
-            j = i - SCORE_LAG
-            if i + 1 < UNITS:
-                project(i + 1)
-            if j >= 0:
-                finish(j, score_pass(j))
-            if t < 2 and b + 1 < B:
-                turn_x(b + 1, t)
-            if i < UNITS:
-                rope("q", i)
-                rope("k", i)
-            if t == 0 and 1 <= b <= B:
-                rot_mx["q", b - 1] = quantise(stage, rot_grouped["q", b - 1], "q_rot")
-                rot_mx["k", b - 1] = quantise(stage, rot_grouped["k", b - 1], "k_rot")
-            if t == 2 and b + 1 < B:
-                x_mx[b + 1] = quantise(stage, x_grouped[b + 1], "x")
+            def quants():
+                if r == 2 and b + 1 < B: quant_x(b + 1, 0)
+                if r == 3 and b + 1 < B: quant_x(b + 1, 1)
+                if 1 <= s <= PAIRS: quant_rot(s - 1)
+            if K["QPOS"] == 0: quants()
+            scs = [(bb, tt, score(bb, tt)) for bb, tt in sched.get(s, [])]
+            if s + 1 < PAIRS: g_side(s + 1)
+            for idx, (bb, tt, sc) in enumerate(scs): finish(bb, tt, sc, onv=K["MASKV"] and tt == 3 and bb % K["MASKV"] == 0)
+            if K["XP"] and r in (0, 1) and b + 1 < B: permute_x(b + 1, r)
+            if r in (1, 2) and b + 1 < B: turn_x(b + 1, r - 1)
+            if s < PAIRS:
+                if not is_w(s, 0):
+                    t_side(s, 0)
+                    s_side(s, 0)
+                v_side(s, 1)
+                if s == 0:
+                    quant_w("q", 0)
+                    quant_w("q", 1)
+                if K["QPOS"] == 1: quants()
+                t_side(s, 1)
+                s_side(s, 1)
+                if is_w(s, 0):
+                    t_side(s, 0)
+                    s_side(s, 0)
+        b = B - 1
+        late = [(b - 1, t) for t in range(TILES) if 4 * (b - 1) + K["LAGS"][t] >= PAIRS and 4 * (b - 1) + K["LAGS"][t] != 32]
+        for bb, t in late + [(b, 0), (b, 1)]:
+            finish(bb, t, score(bb, t))
+        quant_rot(PAIRS - 1)
+        for t in (2, 3):
+            finish(b, t, score(b, t), onv=True)

@@ -19,7 +19,7 @@ TILES = S // P
 INV_SQRT_HD = 1.0 / math.sqrt(HD)
 FLOPS = 2 * (2 * B * S * H * H) + 2 * B * S * S * H
 PAIRS = 4 * B
-K = dict(WJ=0, XP=0, GP="low2", MASKV=0, WEVERY=0, SPLITMASK=1, LAGS=(4, 5, 6, 7), TAILV=1, QPOS=1)
+K = dict(DH=0, DS=0, WADD="V", WJ=0, XP=1, GP="low2", MASKV=0, WEVERY=0, SPLITMASK=1, LAGS=(4, 5, 6, 7), TAILV=1, QPOS=1)
 
 def tile_llamaattention_pa_t_kernel(tc, hidden_states, wq_deq, wk_deq, cos, sin, attention_mask, out):
     nc = tc.nc
@@ -65,6 +65,12 @@ def tile_llamaattention_pa_t_kernel(tc, hidden_states, wq_deq, wk_deq, cos, sin,
                 (sin_table, sin_by_code, slice(HALF_RUN, RUN), 1.0),
             ):
                 nc.scalar.mul(out=table[:, :, :, part], in_=rows[:, :, :, part], mul=sign)
+
+        idle = keep.tile([P, S], BF16)
+        if K["DH"] or K["DS"]: nc.vector.memset(idle[:], 0.0)
+        def dummy():
+            d = psum.tile([P, S], F32, name="dummy", tag="misc", bufs=2)
+            nc.tensor.matmul(out=d[:], lhsT=idle[:, 0:P], rhs=idle[:], start=True, stop=True)
 
         def turn_two_tiles(words, grouped_words, copy_out, tag="misc"):
             bank = psum.tile([P, 2, 2, P], F32, name="bank", tag=tag, bufs=4 if tag == "raw" else 2)
@@ -136,12 +142,17 @@ def tile_llamaattention_pa_t_kernel(tc, hidden_states, wq_deq, wk_deq, cos, sin,
             for part in ("low", "high"):
                 if part not in gparts(s, k):
                     nc.vector.tensor_tensor(out=prod[j][1][:, :, :, PART[part]], in0=view(raw[j][:])[:, :, :, PART[OTHER[part]]], in1=factor(sin_table, j[2], PART[part]), op=MULT)
+            w_add(s, k, False)
+        def w_add(s, k, late):
+            j = jobs(s)[k]
             if is_w(s, k):
+                if K["WADD"] == "V" and not late: return
                 sums[j] = products.tile([P, 2, CHUNKS * RUN, 2], BF16, name="sums", tag="sums")
                 a, c = [x[:].rearrange("p (u e) c f -> p u (c f) e", u=2) for x in prod[j]]
-                for h in range(K["SPLITMASK"]):
-                    hs = slice(h * 2 // K["SPLITMASK"], (h + 1) * 2 // K["SPLITMASK"])
-                    nc.gpsimd.tensor_tensor(out=sums[j][:, hs], in0=a[:, hs], in1=c[:, hs], op=ADD)
+                sm = 1 if late else min(2, K["SPLITMASK"])
+                for h in range(sm):
+                    hs = slice(h * 2 // sm, (h + 1) * 2 // sm)
+                    (nc.vector if late else nc.gpsimd).tensor_tensor(out=sums[j][:, hs], in0=a[:, hs], in1=c[:, hs], op=ADD)
         turned = {}
         def t_side(s, k):
             n, b, t = j = jobs(s)[k]
@@ -190,6 +201,7 @@ def tile_llamaattention_pa_t_kernel(tc, hidden_states, wq_deq, wk_deq, cos, sin,
             f = 2 * h
             turn_two_tiles(w_rows[n][:].bitcast(F32)[:, f : f + 2, :], wg[n][:].rearrange("p n t -> p (n t)").bitcast(F32).rearrange("p (n u) -> p n u", u=2)[:, f * P : (f + 2) * P, :], eng, tag="raw")
         def quant_w(n, h): quantise(w_mx[n], wg[n], 256 * h, 256 * h + 256)
+        for i in range(K["DH"]): dummy()
         turn_w("k", 0, nc.vector.tensor_copy)
         turn_w("k", 1, nc.scalar.copy)
         turn_x(0, 0, nc.vector.tensor_copy)
@@ -224,6 +236,7 @@ def tile_llamaattention_pa_t_kernel(tc, hidden_states, wq_deq, wk_deq, cos, sin,
                 if r == 3 and b + 1 < B: quant_x(b + 1, 1)
                 if 1 <= s <= PAIRS: quant_rot(s - 1)
             if K["QPOS"] == 0: quants()
+            if s < K["DS"]: dummy()
             scs = [(bb, tt, score(bb, tt)) for bb, tt in sched.get(s, [])]
             if s + 1 < PAIRS: g_side(s + 1)
             for idx, (bb, tt, sc) in enumerate(scs): finish(bb, tt, sc, onv=K["MASKV"] and tt == 3 and bb % K["MASKV"] == 0)
@@ -234,6 +247,7 @@ def tile_llamaattention_pa_t_kernel(tc, hidden_states, wq_deq, wk_deq, cos, sin,
                     t_side(s, 0)
                     s_side(s, 0)
                 v_side(s, 1)
+                if K["WADD"] == "V": w_add(s, 0, True)
                 if s == 0:
                     quant_w("q", 0)
                     quant_w("q", 1)

@@ -19,7 +19,7 @@ TILES = S // P
 INV_SQRT_HD = 1.0 / math.sqrt(HD)
 FLOPS = 2 * (2 * B * S * H * H) + 2 * B * S * S * H
 PAIRS = 4 * B
-K = dict(DH=0, DS=0, WADD="V", WJ=0, XP=1, GP="low2", MASKV=0, WEVERY=0, SPLITMASK=1, LAGS=(4, 5, 6, 7), TAILV=1, QPOS=1)
+K = dict(ESPLIT=1, SIN1=0, DH=5, DS=5, WADD="V", WJ=0, XP=1, GP="low2", MASKV=0, WEVERY=0, SPLITMASK=1, LAGS=(4, 5, 6, 7), TAILV=1, QPOS=1)
 
 def tile_llamaattention_pa_t_kernel(tc, hidden_states, wq_deq, wk_deq, cos, sin, attention_mask, out):
     nc = tc.nc
@@ -58,6 +58,7 @@ def tile_llamaattention_pa_t_kernel(tc, hidden_states, wq_deq, wk_deq, cos, sin,
             load_x(b, 0, 4)
         cos_by_code = cos_rows[:].rearrange("p s (f q) -> p s q f", q=PACK)
         sin_by_code = sin_rows[:].rearrange("p s (f q) -> p s q f", q=PACK)
+        sin_wide = keep.tile([P, TILES, PACK * CHUNKS, 2, HALF_RUN], BF16)
         def tables():
             for table, rows, part, sign in (
                 (cos_table, cos_by_code, slice(0, RUN), 1.0),
@@ -65,6 +66,9 @@ def tile_llamaattention_pa_t_kernel(tc, hidden_states, wq_deq, wk_deq, cos, sin,
                 (sin_table, sin_by_code, slice(HALF_RUN, RUN), 1.0),
             ):
                 nc.scalar.mul(out=table[:, :, :, part], in_=rows[:, :, :, part], mul=sign)
+            if K["SIN1"]:
+                for t in range(TILES):
+                    nc.scalar.copy(out=sin_wide[:, t].rearrange("p (q c) h f -> p q c (h f)", c=CHUNKS), in_=sin_table[:, t].unsqueeze(2).to_broadcast([P, PACK, CHUNKS, RUN]))
 
         idle = keep.tile([P, S], BF16)
         if K["DH"] or K["DS"]: nc.vector.memset(idle[:], 0.0)
@@ -135,10 +139,17 @@ def tile_llamaattention_pa_t_kernel(tc, hidden_states, wq_deq, wk_deq, cos, sin,
                 for part in gparts(s, k):
                     tmp = results.tile([P, PACK, CHUNKS, HALF_RUN], F32, name="tmp", tag="tmp")
                     nc.scalar.copy(out=tmp[:], in_=view(raw[j][:])[:, :, :, PART[OTHER[part]]])
-                    nc.gpsimd.tensor_tensor(out=prod[j][1][:][:, :, :, PART[part]], in0=tmp[:], in1=factor(sin_table, j[2], PART[part]), op=MULT)
+                    es = K["ESPLIT"]
+                    for h in range(es):
+                        hs = slice(h * PACK // es, (h + 1) * PACK // es)
+                        nc.gpsimd.tensor_tensor(out=prod[j][1][:][:, hs, :, PART[part]], in0=tmp[:, hs], in1=factor(sin_table, j[2], PART[part])[:, hs], op=MULT)
         def v_side(s, k):
             j = jobs(s)[k]
             nc.vector.tensor_tensor(out=prod[j][0][:], in0=view(raw[j][:]), in1=factor(cos_table, j[2], slice(0, RUN)), op=MULT)
+            if K["SIN1"] and not gparts(s, k):
+                swapped = raw[j][:].rearrange("p (q c h f) -> p q c h f", q=PACK, c=CHUNKS, h=2)[:, :, :, ::-1, :].rearrange("p q c h f -> p (q c) h f")
+                nc.vector.tensor_tensor(out=prod[j][1][:].rearrange("p q c (h f) -> p (q c) h f", h=2), in0=swapped, in1=sin_wide[:, j[2]], op=MULT)
+                return w_add(s, k, False)
             for part in ("low", "high"):
                 if part not in gparts(s, k):
                     nc.vector.tensor_tensor(out=prod[j][1][:, :, :, PART[part]], in0=view(raw[j][:])[:, :, :, PART[OTHER[part]]], in1=factor(sin_table, j[2], PART[part]), op=MULT)

@@ -19,7 +19,7 @@ TILES = S // P
 INV_SQRT_HD = 1.0 / math.sqrt(HD)
 FLOPS = 2 * (2 * B * S * H * H) + 2 * B * S * S * H
 PAIRS = 4 * B
-K = dict(ESPLIT=1, SIN1=0, DH=5, DS=5, WADD="V", WJ=0, XP=1, GP="low2", MASKV=0, WEVERY=0, SPLITMASK=1, LAGS=(4, 5, 6, 7), TAILV=1, QPOS=1)
+K = dict(ACC=0, WE=0, WE0=0, DM=3, EE=0, TI=0, AL=64, ESPLIT=1, SIN1=0, DH=6, DS=2, WADD="V", WJ=0, XP=1, GP="low2", MASKV=0, WEVERY=0, SPLITMASK=1, LAGS=(4, 5, 6, 7), TAILV=1, QPOS=1)
 
 def tile_llamaattention_pa_t_kernel(tc, hidden_states, wq_deq, wk_deq, cos, sin, attention_mask, out):
     nc = tc.nc
@@ -73,7 +73,7 @@ def tile_llamaattention_pa_t_kernel(tc, hidden_states, wq_deq, wk_deq, cos, sin,
         idle = keep.tile([P, S], BF16)
         if K["DH"] or K["DS"]: nc.vector.memset(idle[:], 0.0)
         def dummy():
-            d = psum.tile([P, S], F32, name="dummy", tag="misc", bufs=2)
+            d = psum.tile([P, S], F32, name="dummy", tag="turned", bufs=2)
             nc.tensor.matmul(out=d[:], lhsT=idle[:, 0:P], rhs=idle[:], start=True, stop=True)
 
         def turn_two_tiles(words, grouped_words, copy_out, tag="misc"):
@@ -84,7 +84,7 @@ def tile_llamaattention_pa_t_kernel(tc, hidden_states, wq_deq, wk_deq, cos, sin,
             copy_out(out=grouped_words.rearrange("p (r n) u -> p r n u", r=2), in_=bank[:].rearrange("p r u n -> p r n u"))
 
         def new_mx(pool, tag):
-            return (pool.tile([P, 512], U32, name=tag + "_codes", tag=tag + "_codes", align_bytes=64), pool.tile([P, 512], U8, name=tag + "_scales", tag=tag + "_scales", align_bytes=64))
+            return (pool.tile([P, 512], U32, name=tag + "_codes", tag=tag + "_codes", align_bytes=K["AL"]), pool.tile([P, 512], U8, name=tag + "_scales", tag=tag + "_scales", align_bytes=K["AL"]))
 
         def quantise(mx, grouped, lo, hi):
             nc.vector.quantize_mx(out=mx[0][:, lo:hi].bitcast(FP8X4), scales=mx[1][:, lo:hi], in_=grouped[:, lo:hi].rearrange("p n t -> p (n t)"))
@@ -101,7 +101,7 @@ def tile_llamaattention_pa_t_kernel(tc, hidden_states, wq_deq, wk_deq, cos, sin,
             nc.scalar.copy(out=xp[b, h][:], in_=x_rows[b][:].bitcast(F32)[:, 2*h:2*h+2, :].rearrange("p r (n u) -> p r u n", u=2))
         def turn_x(b, h, eng=None):
             if h == 0:
-                x_g[b] = stage.tile([P, S, PACK], BF16, name="x_g", tag="x_g", align_bytes=64)
+                x_g[b] = stage.tile([P, S, PACK], BF16, name="x_g", tag="x_g", align_bytes=K["AL"])
                 x_mx[b] = new_mx(stage, "x")
             f = 2 * h
             turn_two_tiles(xp[b, h][:] if (b, h) in xp else x_rows[b][:].bitcast(F32)[:, f : f + 2, :], x_g[b][:].rearrange("p n t -> p (n t)").bitcast(F32).rearrange("p (n u) -> p n u", u=2)[:, f * P : (f + 2) * P, :], eng or nc.scalar.copy)
@@ -114,12 +114,14 @@ def tile_llamaattention_pa_t_kernel(tc, hidden_states, wq_deq, wk_deq, cos, sin,
             return [(n, b, 2 * (r % 2)), (n, b, 2 * (r % 2) + 1)]
         def gparts(s, k):
             if is_w(s, k): return []
+            if K["EE"] and s < K["EE"]: return ["low"]
             if K["GP"] == "low2": return ["low"] if k == 1 else []
             if K["GP"] == "none": return []
             if K["GP"] == "low12": return ["low"]
             if K["GP"] == "both2odd": return ["low", "high"] if k == 1 and s % 2 else []
             if K["GP"] == "lowodd": return ["low"] if k == 1 and s % 2 else []
         def is_w(s, k):
+            if K["WE"] and k == 0 and K["WE0"] <= s < K["WE"]: return True
             return K["WJ"] and k == 0 and s % K["WJ"] == K["WJ"] - 1 and s < PAIRS - 2
         sums = {}
         PART = dict(low=slice(0, HALF_RUN), high=slice(HALF_RUN, RUN))
@@ -177,10 +179,17 @@ def tile_llamaattention_pa_t_kernel(tc, hidden_states, wq_deq, wk_deq, cos, sin,
                 for i in (0, 1):
                     nc.tensor.matmul(out=tn[:, c, :], lhsT=prod[j][i][:, c].rearrange("p c f -> p (c f)"), rhs=ident[:], is_transpose=True, start=i == 0, stop=i == 1)
             turned[j] = tn
+        def t_both(s):
+            js = jobs(s)
+            for j in js: turned[j] = psum.tile([P, PACK, P], F32, name="turned", tag="turned", bufs=2)
+            for c in range(PACK):
+                for i in (0, 1):
+                    for j in js:
+                        nc.tensor.matmul(out=turned[j][:, c, :], lhsT=prod[j][i][:, c].rearrange("p c f -> p (c f)"), rhs=ident[:], is_transpose=True, start=i == 0, stop=i == 1)
         def s_side(s, k, eng=None):
             n, b, t = j = jobs(s)[k]
             if (n, b) not in rot_g:
-                rot_g[n, b] = stage.tile([P, S, PACK], BF16, name=n + "_rot", tag=n + "_rot", align_bytes=64)
+                rot_g[n, b] = stage.tile([P, S, PACK], BF16, name=n + "_rot", tag=n + "_rot", align_bytes=K["AL"])
                 rot_mx[n, b] = new_mx(stage, n + "rot")
             if is_w(s, k):
                 (eng or nc.scalar.copy)(out=rot_g[n, b][:].rearrange("p n t -> p (n t)").bitcast(F32).rearrange("p (n u) -> p n u", u=2)[:, t * P : (t + 1) * P, :], in_=turned[j][:, 0:2].rearrange("p c n -> p n c"))
@@ -197,6 +206,11 @@ def tile_llamaattention_pa_t_kernel(tc, hidden_states, wq_deq, wk_deq, cos, sin,
             res = results.tile([P, S], F32, name="res", tag="res")
             if onv:
                 nc.vector.scalar_tensor_tensor(out=res[:], in0=sc[:], scalar=INV_SQRT_HD, in1=mask_rows[:, t, :], op0=MULT, op1=ADD)
+            elif K["ACC"]:
+                nc.scalar.mul(out=res[:], in_=sc[:], mul=INV_SQRT_HD)
+                nc.sync.dma_start(out=out[b, t * P : (t + 1) * P, :], in_=res[:])
+                if t == 3: nc.gpsimd.dma_start(out=out[b].rearrange("(t p) k -> p t k", p=P), in_=mask_f32[:], accum_op=ADD)
+                return
             else:
                 nc.scalar.mul(out=res[:], in_=sc[:], mul=INV_SQRT_HD)
                 w = S // K["SPLITMASK"]
@@ -207,7 +221,7 @@ def tile_llamaattention_pa_t_kernel(tc, hidden_states, wq_deq, wk_deq, cos, sin,
         wg = {}
         def turn_w(n, h, eng):
             if h == 0:
-                wg[n] = keep.tile([P, H, PACK], BF16, name=n + "_w_g", tag=n + "_w_g", align_bytes=64)
+                wg[n] = keep.tile([P, H, PACK], BF16, name=n + "_w_g", tag=n + "_w_g", align_bytes=K["AL"])
                 w_mx[n] = new_mx(keep, n + "_w")
             f = 2 * h
             turn_two_tiles(w_rows[n][:].bitcast(F32)[:, f : f + 2, :], wg[n][:].rearrange("p n t -> p (n t)").bitcast(F32).rearrange("p (n u) -> p n u", u=2)[:, f * P : (f + 2) * P, :], eng, tag="raw")
@@ -221,11 +235,14 @@ def tile_llamaattention_pa_t_kernel(tc, hidden_states, wq_deq, wk_deq, cos, sin,
         quant_w("k", 1)
         quant_x(0, 0)
         tables()
+        for i in range(K["DM"]): dummy()
         project(0)
         turn_w("q", 0, nc.scalar.copy)
         turn_w("q", 1, nc.scalar.copy)
         g_side(0)
-        pending = []
+        if K["ACC"]:
+            mask_f32 = keep.tile([P, TILES, S], F32)
+            nc.gpsimd.tensor_copy(out=mask_f32[:], in_=mask_rows[:])
         sched = {}
         for b in range(B):
             for t in range(TILES):
@@ -254,7 +271,7 @@ def tile_llamaattention_pa_t_kernel(tc, hidden_states, wq_deq, wk_deq, cos, sin,
             if K["XP"] and r in (0, 1) and b + 1 < B: permute_x(b + 1, r)
             if r in (1, 2) and b + 1 < B: turn_x(b + 1, r - 1)
             if s < PAIRS:
-                if not is_w(s, 0):
+                if not is_w(s, 0) and not K["TI"]:
                     t_side(s, 0)
                     s_side(s, 0)
                 v_side(s, 1)
@@ -263,7 +280,10 @@ def tile_llamaattention_pa_t_kernel(tc, hidden_states, wq_deq, wk_deq, cos, sin,
                     quant_w("q", 0)
                     quant_w("q", 1)
                 if K["QPOS"] == 1: quants()
-                t_side(s, 1)
+                if K["TI"]:
+                    t_both(s)
+                    s_side(s, 0)
+                else: t_side(s, 1)
                 s_side(s, 1)
                 if is_w(s, 0):
                     t_side(s, 0)
@@ -274,4 +294,4 @@ def tile_llamaattention_pa_t_kernel(tc, hidden_states, wq_deq, wk_deq, cos, sin,
             finish(bb, t, score(bb, t))
         quant_rot(PAIRS - 1)
         for t in (2, 3):
-            finish(b, t, score(b, t), onv=True)
+            finish(b, t, score(b, t), onv=not K["ACC"])

@@ -19,7 +19,7 @@ TILES = S // P
 INV_SQRT_HD = 1.0 / math.sqrt(HD)
 FLOPS = 2 * (2 * B * S * H * H) + 2 * B * S * S * H
 PAIRS = 4 * B
-K = dict(ACC=0, WE=0, WE0=0, DM=3, EE=0, TI=0, AL=64, ESPLIT=1, SIN1=0, DH=6, DS=2, WADD="V", WJ=0, XP=1, GP="low2", MASKV=0, WEVERY=0, SPLITMASK=1, LAGS=(4, 5, 6, 7), TAILV=1, QPOS=1)
+K = dict(TAIL=2, HEAD=1, TG=1, SF=0, MF=0, ACC=0, WE=0, WE0=0, DM=6, EE=0, TI=0, AL=64, ESPLIT=1, SIN1=0, DH=10, DS=0, WADD="V", WJ=0, XP=1, GP="low2", MASKV=0, WEVERY=0, SPLITMASK=1, LAGS=(4, 5, 6, 7), TAILV=1, QPOS=1)
 
 def tile_llamaattention_pa_t_kernel(tc, hidden_states, wq_deq, wk_deq, cos, sin, attention_mask, out):
     nc = tc.nc
@@ -59,22 +59,22 @@ def tile_llamaattention_pa_t_kernel(tc, hidden_states, wq_deq, wk_deq, cos, sin,
         cos_by_code = cos_rows[:].rearrange("p s (f q) -> p s q f", q=PACK)
         sin_by_code = sin_rows[:].rearrange("p s (f q) -> p s q f", q=PACK)
         sin_wide = keep.tile([P, TILES, PACK * CHUNKS, 2, HALF_RUN], BF16)
-        def tables():
+        def tables(t0=0, t1=TILES):
             for table, rows, part, sign in (
                 (cos_table, cos_by_code, slice(0, RUN), 1.0),
                 (sin_table, sin_by_code, slice(0, HALF_RUN), -1.0),
                 (sin_table, sin_by_code, slice(HALF_RUN, RUN), 1.0),
             ):
-                nc.scalar.mul(out=table[:, :, :, part], in_=rows[:, :, :, part], mul=sign)
+                nc.scalar.mul(out=table[:, t0:t1, :, part], in_=rows[:, t0:t1, :, part], mul=sign)
             if K["SIN1"]:
                 for t in range(TILES):
                     nc.scalar.copy(out=sin_wide[:, t].rearrange("p (q c) h f -> p q c (h f)", c=CHUNKS), in_=sin_table[:, t].unsqueeze(2).to_broadcast([P, PACK, CHUNKS, RUN]))
 
-        idle = keep.tile([P, S], BF16)
+        idle = keep.tile([P, P], BF16)
         if K["DH"] or K["DS"]: nc.vector.memset(idle[:], 0.0)
         def dummy():
             d = psum.tile([P, S], F32, name="dummy", tag="turned", bufs=2)
-            nc.tensor.matmul(out=d[:], lhsT=idle[:, 0:P], rhs=idle[:], start=True, stop=True)
+            nc.tensor.matmul(out=d[:, 0:P], lhsT=idle[:], rhs=idle[:], start=True, stop=True)
 
         def turn_two_tiles(words, grouped_words, copy_out, tag="misc"):
             bank = psum.tile([P, 2, 2, P], F32, name="bank", tag=tag, bufs=4 if tag == "raw" else 2)
@@ -116,6 +116,9 @@ def tile_llamaattention_pa_t_kernel(tc, hidden_states, wq_deq, wk_deq, cos, sin,
             if is_w(s, k): return []
             if K["EE"] and s < K["EE"]: return ["low"]
             if K["GP"] == "low2": return ["low"] if k == 1 else []
+            if K["GP"] == "low1": return ["low"] if k == 0 else []
+            if K["GP"] == "both1odd": return ["low", "high"] if k == 0 and s % 2 else []
+            if K["GP"] == "both2even": return ["low", "high"] if k == 1 and s % 2 == 0 else []
             if K["GP"] == "none": return []
             if K["GP"] == "low12": return ["low"]
             if K["GP"] == "both2odd": return ["low", "high"] if k == 1 and s % 2 else []
@@ -145,9 +148,10 @@ def tile_llamaattention_pa_t_kernel(tc, hidden_states, wq_deq, wk_deq, cos, sin,
                     for h in range(es):
                         hs = slice(h * PACK // es, (h + 1) * PACK // es)
                         nc.gpsimd.tensor_tensor(out=prod[j][1][:][:, hs, :, PART[part]], in0=tmp[:, hs], in1=factor(sin_table, j[2], PART[part])[:, hs], op=MULT)
-        def v_side(s, k):
+        def v_side(s, k, between=None):
             j = jobs(s)[k]
             nc.vector.tensor_tensor(out=prod[j][0][:], in0=view(raw[j][:]), in1=factor(cos_table, j[2], slice(0, RUN)), op=MULT)
+            if between: between()
             if K["SIN1"] and not gparts(s, k):
                 swapped = raw[j][:].rearrange("p (q c h f) -> p q c h f", q=PACK, c=CHUNKS, h=2)[:, :, :, ::-1, :].rearrange("p q c h f -> p (q c) h f")
                 nc.vector.tensor_tensor(out=prod[j][1][:].rearrange("p q c (h f) -> p (q c) h f", h=2), in0=swapped, in1=sin_wide[:, j[2]], op=MULT)
@@ -173,6 +177,12 @@ def tile_llamaattention_pa_t_kernel(tc, hidden_states, wq_deq, wk_deq, cos, sin,
             if is_w(s, k):
                 for u in range(2):
                     nc.tensor.transpose(tn[:, u, :], sums[j][:].rearrange("p u n e -> p (u n e)").bitcast(F32)[:, u * P : u * P + P], ident[:])
+                turned[j] = tn
+                return
+            if K["TG"]:
+                for i in (0, 1):
+                    for c in range(PACK):
+                        nc.tensor.matmul(out=tn[:, c, :], lhsT=prod[j][i][:, c].rearrange("p c f -> p (c f)"), rhs=ident[:], is_transpose=True, start=i == 0 and c == 0, stop=i == 1 and c == PACK - 1)
                 turned[j] = tn
                 return
             for c in range(PACK):
@@ -227,16 +237,29 @@ def tile_llamaattention_pa_t_kernel(tc, hidden_states, wq_deq, wk_deq, cos, sin,
             turn_two_tiles(w_rows[n][:].bitcast(F32)[:, f : f + 2, :], wg[n][:].rearrange("p n t -> p (n t)").bitcast(F32).rearrange("p (n u) -> p n u", u=2)[:, f * P : (f + 2) * P, :], eng, tag="raw")
         def quant_w(n, h): quantise(w_mx[n], wg[n], 256 * h, 256 * h + 256)
         for i in range(K["DH"]): dummy()
-        turn_w("k", 0, nc.vector.tensor_copy)
-        turn_w("k", 1, nc.scalar.copy)
-        turn_x(0, 0, nc.vector.tensor_copy)
-        turn_x(0, 1)
-        quant_w("k", 0)
-        quant_w("k", 1)
-        quant_x(0, 0)
-        tables()
-        for i in range(K["DM"]): dummy()
-        project(0)
+        if K["HEAD"]:
+            turn_w("k", 0, nc.vector.tensor_copy)
+            turn_w("k", 1, nc.scalar.copy)
+            turn_x(0, 0)
+            turn_x(0, 1)
+            quant_w("k", 0)
+            quant_w("k", 1)
+            quant_x(0, 0)
+            tables(0, 2)
+            for i in range(K["DM"]): dummy()
+            project(0)
+            tables(2, 4)
+        else:
+            turn_w("k", 0, nc.vector.tensor_copy)
+            turn_w("k", 1, nc.scalar.copy)
+            turn_x(0, 0, nc.vector.tensor_copy)
+            turn_x(0, 1)
+            quant_w("k", 0)
+            quant_w("k", 1)
+            quant_x(0, 0)
+            tables()
+            for i in range(K["DM"]): dummy()
+            project(0)
         turn_w("q", 0, nc.scalar.copy)
         turn_w("q", 1, nc.scalar.copy)
         g_side(0)
@@ -255,21 +278,26 @@ def tile_llamaattention_pa_t_kernel(tc, hidden_states, wq_deq, wk_deq, cos, sin,
             if s == 0:
                 v_side(s, 0)
                 quant_x(0, 1)
+            if K["SF"]:
+                scs = [(bb, tt, score(bb, tt)) for bb, tt in sched.get(s, [])]
             if s + 1 < PAIRS:
                 project(s + 1)
-            if 0 < s < PAIRS: v_side(s, 0)
-
+            ql = 2 if K["QPOS"] == 2 else 1
             def quants():
                 if r == 2 and b + 1 < B: quant_x(b + 1, 0)
                 if r == 3 and b + 1 < B: quant_x(b + 1, 1)
-                if 1 <= s <= PAIRS: quant_rot(s - 1)
+                if s >= ql: quant_rot(s - ql)
+            if 0 < s < PAIRS: v_side(s, 0, quants if K["QPOS"] == 2 else None)
             if K["QPOS"] == 0: quants()
             if s < K["DS"]: dummy()
-            scs = [(bb, tt, score(bb, tt)) for bb, tt in sched.get(s, [])]
-            if s + 1 < PAIRS: g_side(s + 1)
+            if not K["SF"]: scs = [(bb, tt, score(bb, tt)) for bb, tt in sched.get(s, [])]
+            if s + 1 < PAIRS and not K["MF"]: g_side(s + 1)
             for idx, (bb, tt, sc) in enumerate(scs): finish(bb, tt, sc, onv=K["MASKV"] and tt == 3 and bb % K["MASKV"] == 0)
-            if K["XP"] and r in (0, 1) and b + 1 < B: permute_x(b + 1, r)
-            if r in (1, 2) and b + 1 < B: turn_x(b + 1, r - 1)
+            if s + 1 < PAIRS and K["MF"]: g_side(s + 1)
+            if K["XP"] and K["QPOS"] != 2 and r in (0, 1) and b + 1 < B: permute_x(b + 1, r)
+            if K["XP"] and K["QPOS"] == 2 and r in (2, 3) and b + 2 < B: permute_x(b + 2, r - 2)
+            xr = (0, 1) if K["QPOS"] == 2 else (1, 2)
+            if r in xr and b + 1 < B: turn_x(b + 1, r - xr[0])
             if s < PAIRS:
                 if not is_w(s, 0) and not K["TI"]:
                     t_side(s, 0)
@@ -288,10 +316,25 @@ def tile_llamaattention_pa_t_kernel(tc, hidden_states, wq_deq, wk_deq, cos, sin,
                 if is_w(s, 0):
                     t_side(s, 0)
                     s_side(s, 0)
+        if K["QPOS"] == 2: quant_rot(PAIRS - 2)
         b = B - 1
         late = [(b - 1, t) for t in range(TILES) if 4 * (b - 1) + K["LAGS"][t] >= PAIRS and 4 * (b - 1) + K["LAGS"][t] != 32]
-        for bb, t in late + [(b, 0), (b, 1)]:
-            finish(bb, t, score(bb, t))
-        quant_rot(PAIRS - 1)
-        for t in (2, 3):
-            finish(b, t, score(b, t), onv=not K["ACC"])
+        if K["TAIL"]:
+            for bb, t in late: finish(bb, t, score(bb, t))
+            if K["TAIL"] == 2:
+                ss = [score(b, 0), score(b, 1)]
+                finish(b, 0, ss[0])
+                quantise(rot_mx["q", b], rot_g["q", b], 2 * P, 3 * P)
+                finish(b, 1, ss[1], onv=True)
+                quantise(rot_mx["q", b], rot_g["q", b], 3 * P, 4 * P)
+            else:
+                finish(b, 0, score(b, 0))
+                finish(b, 1, score(b, 1), onv=True)
+                quant_rot(PAIRS - 1)
+            for t in (2, 3): finish(b, t, score(b, t), onv=True)
+        else:
+            for bb, t in late + [(b, 0), (b, 1)]:
+                finish(bb, t, score(bb, t))
+            quant_rot(PAIRS - 1)
+            for t in (2, 3):
+                finish(b, t, score(b, t), onv=not K["ACC"])

@@ -19,7 +19,7 @@ TILES = S // P
 INV_SQRT_HD = 1.0 / math.sqrt(HD)
 FLOPS = 2 * (2 * B * S * H * H) + 2 * B * S * S * H
 PAIRS = 4 * B
-K = dict(TAIL=2, HEAD=1, TG=1, SF=0, MF=0, ACC=0, WE=0, WE0=0, DM=6, EE=0, TI=0, AL=64, ESPLIT=1, SIN1=0, DH=10, DS=0, WADD="V", WJ=0, XP=1, GP="low2", MASKV=0, WEVERY=0, SPLITMASK=1, LAGS=(4, 5, 6, 7), TAILV=1, QPOS=1)
+K = dict(GX=(), TOK=0, WP=(3,), WQ=0, SMID=0, TAIL=2, HEAD=1, TG=1, SF=0, MF=0, ACC=0, WE=0, WE0=0, DM=6, EE=0, TI=0, AL=64, ESPLIT=1, SIN1=1, DH=10, DS=0, WADD="V", WJ=0, XP=1, GP="low2", MASKV=0, WEVERY=0, SPLITMASK=1, LAGS=(4, 5, 6, 7), TAILV=1, QPOS=1)
 
 def tile_llamaattention_pa_t_kernel(tc, hidden_states, wq_deq, wk_deq, cos, sin, attention_mask, out):
     nc = tc.nc
@@ -66,9 +66,8 @@ def tile_llamaattention_pa_t_kernel(tc, hidden_states, wq_deq, wk_deq, cos, sin,
                 (sin_table, sin_by_code, slice(HALF_RUN, RUN), 1.0),
             ):
                 nc.scalar.mul(out=table[:, t0:t1, :, part], in_=rows[:, t0:t1, :, part], mul=sign)
-            if K["SIN1"]:
-                for t in range(TILES):
-                    nc.scalar.copy(out=sin_wide[:, t].rearrange("p (q c) h f -> p q c (h f)", c=CHUNKS), in_=sin_table[:, t].unsqueeze(2).to_broadcast([P, PACK, CHUNKS, RUN]))
+        def widen(t):
+            nc.scalar.copy(out=sin_wide[:, t].rearrange("p (q c) h f -> p q c (h f)", c=CHUNKS), in_=sin_table[:, t].unsqueeze(2).to_broadcast([P, PACK, CHUNKS, RUN]))
 
         idle = keep.tile([P, P], BF16)
         if K["DH"] or K["DS"]: nc.vector.memset(idle[:], 0.0)
@@ -89,9 +88,9 @@ def tile_llamaattention_pa_t_kernel(tc, hidden_states, wq_deq, wk_deq, cos, sin,
         def quantise(mx, grouped, lo, hi):
             nc.vector.quantize_mx(out=mx[0][:, lo:hi].bitcast(FP8X4), scales=mx[1][:, lo:hi], in_=grouped[:, lo:hi].rearrange("p n t -> p (n t)"))
 
-        def mx_pass(acc, st, t, mov):
-            cols = slice(t * P, (t + 1) * P)
-            nc.tensor.matmul_mx(out=acc, lhsT=st[0][:, cols].bitcast(FP8X4), lhsT_scale=st[1][:, cols], rhs=mov[0][:].bitcast(FP8X4), rhs_scale=mov[1][:], start=True, stop=True)
+        def mx_pass(acc, st, c0, mov, m0):
+            cols, mc = slice(c0, c0 + P), slice(m0, m0 + 512)
+            nc.tensor.matmul_mx(out=acc, lhsT=st[0][:, cols].bitcast(FP8X4), lhsT_scale=st[1][:, cols], rhs=mov[0][:, mc].bitcast(FP8X4), rhs_scale=mov[1][:, mc], start=True, stop=True)
 
         w_mx, x_g, x_mx, raw, rot_g, rot_mx, prod = {}, {}, {}, {}, {}, {}, {}
 
@@ -99,14 +98,18 @@ def tile_llamaattention_pa_t_kernel(tc, hidden_states, wq_deq, wk_deq, cos, sin,
         def permute_x(b, h):
             xp[b, h] = stage.tile([P, 2, 2, P], F32, name="xp", tag="xp")
             nc.scalar.copy(out=xp[b, h][:], in_=x_rows[b][:].bitcast(F32)[:, 2*h:2*h+2, :].rearrange("p r (n u) -> p r u n", u=2))
+        kx_g, kx_mx = {}, {}
+        X_COL = (0, 768)
+        def stage_kx(b):
+            kx_g[b] = stage.tile([P, 1024, PACK], BF16, name="kx_g", tag="kx_g", align_bytes=K["AL"])
+            kx_mx[b] = (stage.tile([P, 1024], U32, name="kx_codes", tag="kx_codes", bufs=3, align_bytes=K["AL"]), stage.tile([P, 1024], U8, name="kx_scales", tag="kx_scales", bufs=3, align_bytes=K["AL"]))
         def turn_x(b, h, eng=None):
             if h == 0:
-                x_g[b] = stage.tile([P, S, PACK], BF16, name="x_g", tag="x_g", align_bytes=K["AL"])
-                x_mx[b] = new_mx(stage, "x")
+                stage_kx(b - 1)
             f = 2 * h
-            turn_two_tiles(xp[b, h][:] if (b, h) in xp else x_rows[b][:].bitcast(F32)[:, f : f + 2, :], x_g[b][:].rearrange("p n t -> p (n t)").bitcast(F32).rearrange("p (n u) -> p n u", u=2)[:, f * P : (f + 2) * P, :], eng or nc.scalar.copy)
+            turn_two_tiles(xp[b, h][:] if (b, h) in xp else x_rows[b][:].bitcast(F32)[:, f : f + 2, :], kx_g[b - 1][:].rearrange("p n t -> p (n t)").bitcast(F32).rearrange("p (n u) -> p n u", u=2)[:, X_COL[h] : X_COL[h] + 256, :], eng or nc.scalar.copy)
         def quant_x(b, h):
-            quantise(x_mx[b], x_g[b], h * 256, h * 256 + 256)
+            quantise(kx_mx[b - 1], kx_g[b - 1], X_COL[h], X_COL[h] + 256)
 
         def jobs(s):
             b, r = divmod(s, 4)
@@ -116,6 +119,7 @@ def tile_llamaattention_pa_t_kernel(tc, hidden_states, wq_deq, wk_deq, cos, sin,
             if is_w(s, k): return []
             if K["EE"] and s < K["EE"]: return ["low"]
             if K["GP"] == "low2": return ["low"] if k == 1 else []
+            if K["GP"] == "mix": return [] if k == 0 else (["low", "high"] if s % 4 in K["GX"] else ["low"])
             if K["GP"] == "low1": return ["low"] if k == 0 else []
             if K["GP"] == "both1odd": return ["low", "high"] if k == 0 and s % 2 else []
             if K["GP"] == "both2even": return ["low", "high"] if k == 1 and s % 2 == 0 else []
@@ -125,7 +129,7 @@ def tile_llamaattention_pa_t_kernel(tc, hidden_states, wq_deq, wk_deq, cos, sin,
             if K["GP"] == "lowodd": return ["low"] if k == 1 and s % 2 else []
         def is_w(s, k):
             if K["WE"] and k == 0 and K["WE0"] <= s < K["WE"]: return True
-            return K["WJ"] and k == 0 and s % K["WJ"] == K["WJ"] - 1 and s < PAIRS - 2
+            return K["WJ"] and k == 0 and s % K["WJ"] in K["WP"] and 0 < s < PAIRS - 2
         sums = {}
         PART = dict(low=slice(0, HALF_RUN), high=slice(HALF_RUN, RUN))
         OTHER = dict(low="high", high="low")
@@ -133,17 +137,25 @@ def tile_llamaattention_pa_t_kernel(tc, hidden_states, wq_deq, wk_deq, cos, sin,
         def project(s):
             for j in jobs(s):
                 raw[j] = psum.tile([P, H], F32, name="raw", tag="raw", bufs=4)
-                mx_pass(raw[j][:], x_mx[j[1]], j[2], w_mx[j[0]])
+                mx_pass(raw[j][:], kx_mx[j[1] - 1], X_COL[j[2] // 2] + j[2] % 2 * P, w_mx[j[0]], 0)
         def view(ap): return ap.rearrange("p (q c f) -> p q c f", q=PACK, c=CHUNKS)
         def factor(table, t, part):
             f = table[:, t, :, part]
             return f.unsqueeze(2).to_broadcast([P, PACK, CHUNKS, f.shape[2]])
-        def g_side(s):
+        tmps = {}
+        def g_late(s, tok=False):
+            for k, j in enumerate(jobs(s)):
+                for n, part in enumerate(gparts(s, k)):
+                    if tok and n == 0: nc.vector.memset(prod[j][1][:, 0, 0, 0:1] if part == "low" else prod[j][1][:, 0, 0, HALF_RUN : HALF_RUN + 1], 0.0)
+                    nc.gpsimd.tensor_tensor(out=prod[j][1][:][:, :, :, PART[part]], in0=tmps[j, part][:], in1=factor(sin_table, j[2], PART[part]), op=MULT)
+        def g_side(s, late=False):
             for k, j in enumerate(jobs(s)):
                 prod[j] = (products.tile([P, PACK, CHUNKS, RUN], F32, name="straight", tag="straight"), products.tile([P, PACK, CHUNKS, RUN], F32, name="crossed", tag="crossed"))
                 for part in gparts(s, k):
                     tmp = results.tile([P, PACK, CHUNKS, HALF_RUN], F32, name="tmp", tag="tmp")
                     nc.scalar.copy(out=tmp[:], in_=view(raw[j][:])[:, :, :, PART[OTHER[part]]])
+                    tmps[j, part] = tmp
+                    if late: continue
                     es = K["ESPLIT"]
                     for h in range(es):
                         hs = slice(h * PACK // es, (h + 1) * PACK // es)
@@ -152,7 +164,7 @@ def tile_llamaattention_pa_t_kernel(tc, hidden_states, wq_deq, wk_deq, cos, sin,
             j = jobs(s)[k]
             nc.vector.tensor_tensor(out=prod[j][0][:], in0=view(raw[j][:]), in1=factor(cos_table, j[2], slice(0, RUN)), op=MULT)
             if between: between()
-            if K["SIN1"] and not gparts(s, k):
+            if K["SIN1"] and not gparts(s, k) and s >= 2:
                 swapped = raw[j][:].rearrange("p (q c h f) -> p q c h f", q=PACK, c=CHUNKS, h=2)[:, :, :, ::-1, :].rearrange("p q c h f -> p (q c) h f")
                 nc.vector.tensor_tensor(out=prod[j][1][:].rearrange("p q c (h f) -> p (q c) h f", h=2), in0=swapped, in1=sin_wide[:, j[2]], op=MULT)
                 return w_add(s, k, False)
@@ -199,19 +211,35 @@ def tile_llamaattention_pa_t_kernel(tc, hidden_states, wq_deq, wk_deq, cos, sin,
         def s_side(s, k, eng=None):
             n, b, t = j = jobs(s)[k]
             if (n, b) not in rot_g:
-                rot_g[n, b] = stage.tile([P, S, PACK], BF16, name=n + "_rot", tag=n + "_rot", align_bytes=K["AL"])
-                rot_mx[n, b] = new_mx(stage, n + "rot")
+                if n == "q":
+                    rot_g[n, b] = stage.tile([P, S, PACK], BF16, name=n + "_rot", tag=n + "_rot", align_bytes=K["AL"])
+                    rot_mx[n, b] = new_mx(stage, n + "rot")
+                else:
+                    if b not in kx_g: stage_kx(b)
+                    rot_g[n, b] = kx_g[b][:, 256:768]
             if is_w(s, k):
-                (eng or nc.scalar.copy)(out=rot_g[n, b][:].rearrange("p n t -> p (n t)").bitcast(F32).rearrange("p (n u) -> p n u", u=2)[:, t * P : (t + 1) * P, :], in_=turned[j][:, 0:2].rearrange("p c n -> p n c"))
+                (eng or nc.scalar.copy)(out=rot_g[n, b][:, :, :].rearrange("p n t -> p (n t)").bitcast(F32).rearrange("p (n u) -> p n u", u=2)[:, t * P : (t + 1) * P, :], in_=turned[j][:, 0:2].rearrange("p c n -> p n c"))
                 return
             (eng or nc.scalar.copy)(out=rot_g[n, b][:, t * P : (t + 1) * P, :], in_=turned[j][:].rearrange("p c n -> p n c"))
         def quant_rot(s):
             n, b, t = jobs(s)[0]
-            quantise(rot_mx[n, b], rot_g[n, b], t * P, t * P + 256)
+            if n == "q":
+                quantise(rot_mx[n, b], rot_g[n, b], t * P, t * P + 256)
+            else:
+                lo, hi = (0, 512) if t == 0 else (512, 1024)
+                if b == B - 1: lo, hi = max(lo, 256), min(hi, 768)
+                quantise(kx_mx[b], kx_g[b], lo, hi)
         def score(b, t):
             sc = psum.tile([P, S], F32, name="scores", tag="misc", bufs=2)
-            mx_pass(sc[:], rot_mx["q", b], t, rot_mx["k", b])
+            mx_pass(sc[:], rot_mx["q", b], t * P, kx_mx[b], 256)
             return sc
+        def scale(b, t, sc):
+            res = results.tile([P, S], F32, name="res", tag="res")
+            nc.scalar.mul(out=res[:], in_=sc[:], mul=INV_SQRT_HD)
+            return b, t, res
+        def add_mask(b, t, res):
+            nc.gpsimd.tensor_tensor(out=res[:], in0=res[:], in1=mask_rows[:, t, :], op=ADD)
+            nc.sync.dma_start(out=out[b, t * P : (t + 1) * P, :], in_=res[:])
         def finish(b, t, sc, onv=False):
             res = results.tile([P, S], F32, name="res", tag="res")
             if onv:
@@ -284,35 +312,47 @@ def tile_llamaattention_pa_t_kernel(tc, hidden_states, wq_deq, wk_deq, cos, sin,
                 project(s + 1)
             ql = 2 if K["QPOS"] == 2 else 1
             def quants():
-                if r == 2 and b + 1 < B: quant_x(b + 1, 0)
-                if r == 3 and b + 1 < B: quant_x(b + 1, 1)
                 if s >= ql: quant_rot(s - ql)
             if 0 < s < PAIRS: v_side(s, 0, quants if K["QPOS"] == 2 else None)
             if K["QPOS"] == 0: quants()
             if s < K["DS"]: dummy()
-            if not K["SF"]: scs = [(bb, tt, score(bb, tt)) for bb, tt in sched.get(s, [])]
-            if s + 1 < PAIRS and not K["MF"]: g_side(s + 1)
+            if not K["SF"] and not K["SMID"]: scs = [(bb, tt, score(bb, tt)) for bb, tt in sched.get(s, [])]
+            if K["SMID"]: scs = []
+            if K["TOK"]:
+                if s + 1 < PAIRS: g_side(s + 1, True)
+                held = [scale(*x) for x in scs]
+                scs = []
+            elif s + 1 < PAIRS and not K["MF"]: g_side(s + 1)
             for idx, (bb, tt, sc) in enumerate(scs): finish(bb, tt, sc, onv=K["MASKV"] and tt == 3 and bb % K["MASKV"] == 0)
             if s + 1 < PAIRS and K["MF"]: g_side(s + 1)
-            if K["XP"] and K["QPOS"] != 2 and r in (0, 1) and b + 1 < B: permute_x(b + 1, r)
-            if K["XP"] and K["QPOS"] == 2 and r in (2, 3) and b + 2 < B: permute_x(b + 2, r - 2)
-            xr = (0, 1) if K["QPOS"] == 2 else (1, 2)
+            if K["XP"] and r in (2, 3) and b + 2 < B: permute_x(b + 2, r - 2)
+            xr = (0, 1)
             if r in xr and b + 1 < B: turn_x(b + 1, r - xr[0])
             if s < PAIRS:
                 if not is_w(s, 0) and not K["TI"]:
                     t_side(s, 0)
                     s_side(s, 0)
+                if K["SMID"]:
+                    for bb, tt in sched.get(s, []): finish(bb, tt, score(bb, tt))
                 v_side(s, 1)
-                if K["WADD"] == "V": w_add(s, 0, True)
+                if K["WADD"] == "V" and not K["WQ"]: w_add(s, 0, True)
                 if s == 0:
                     quant_w("q", 0)
                     quant_w("q", 1)
                 if K["QPOS"] == 1: quants()
+                if K["WADD"] == "V" and K["WQ"]: w_add(s, 0, True)
+                if K["TOK"]:
+                    if K["TOK"] == 2 and held:
+                        add_mask(*held[0])
+                        held = held[1:]
+                    if s + 1 < PAIRS: g_late(s + 1, K["TOK"] != 3)
+                    for x in held: add_mask(*x)
                 if K["TI"]:
                     t_both(s)
                     s_side(s, 0)
                 else: t_side(s, 1)
                 s_side(s, 1)
+                if K["SIN1"] and s < 2: widen(2 * s)
                 if is_w(s, 0):
                     t_side(s, 0)
                     s_side(s, 0)

from contextlib import ExitStack
import math
import concourse.mybir as mybir
from concourse.masks import make_identity
F32 = mybir.dt.float32
BF16 = mybir.dt.bfloat16
U32 = mybir.dt.uint32
U8 = mybir.dt.uint8
FP8X4 = mybir.dt.float8_e4m3fn_x4
MULT = mybir.AluOpType.mult
ADD = mybir.AluOpType.add
P = 128
B, S, H, HD = 8, 512, 512, 128
CHUNKS = H // HD
PACK = 4
RUN = HD // PACK
HALF_RUN = RUN // 2
TILES = S // P
INV_SQRT_HD = 1.0 / math.sqrt(HD)
FLOPS = 2 * (2 * B * S * H * H) + 2 * B * S * S * H
PAIRS = 4 * B
K = dict(GX=(), TOK=0, WP=(3,), WQ=0, SMID=0, TAIL=2, HEAD=1, TG=1, SF=0, MF=0, ACC=0, WE=0, WE0=0, DM=6, EE=0, TI=0, AL=64, ESPLIT=1, SIN1=1, DH=10, DS=0, WADD="V", WJ=0, XP=1, GP="low2", MASKV=0, WEVERY=0, SPLITMASK=1, LAGS=(4, 5, 6, 7), TAILV=1, QPOS=1)

def tile_llamaattention_pa_t_kernel(tc, hidden_states, wq_deq, wk_deq, cos, sin, attention_mask, out):
    nc = tc.nc
    with ExitStack() as ctx:
        keep = ctx.enter_context(tc.tile_pool(name="keep", bufs=1))
        stage = ctx.enter_context(tc.tile_pool(name="stage", bufs=2))
        products = ctx.enter_context(tc.tile_pool(name="products", bufs=4))
        results = ctx.enter_context(tc.tile_pool(name="results", bufs=6))
        psum = ctx.enter_context(tc.psum_pool(name="psum", bufs=1))
        ctx.enter_context(tc.manual_schedule())
        w_rows = {n: keep.tile([P, TILES, H], BF16, name="w_rows" + n) for n in "qk"}
        x_rows = [keep.tile([P, TILES, H], BF16, name="x_rows%d" % b) for b in range(B)]
        cos_rows = keep.tile([P, TILES, HD], BF16)
        sin_rows = keep.tile([P, TILES, HD], BF16)
        cos_table = keep.tile([P, TILES, PACK, RUN], BF16)
        sin_table = keep.tile([P, TILES, PACK, RUN], BF16)
        mask_rows = keep.tile([P, TILES, S], BF16)
        ident = keep.tile([P, P], F32)
        make_identity(nc, ident[:])

        def load_w(n, w, h):
            nc.sync.dma_start(out=w_rows[n][:, 2*h:2*h+2], in_=w.rearrange("(p t) k -> p t k", p=P)[:, 2*h:2*h+2])
        def load_x(b, t0, t1):
            nc.sync.dma_start(out=x_rows[b][:, t0:t1], in_=hidden_states[b].rearrange("(t p) k -> p t k", p=P)[:, t0:t1])
        load_w("k", wk_deq, 0)
        load_w("k", wk_deq, 1)
        load_x(0, 0, 2)
        load_x(0, 2, 4)
        nc.sync.dma_start(out=cos_rows[:], in_=cos.rearrange("(t p) f -> p t f", p=P))
        nc.sync.dma_start(out=sin_rows[:], in_=sin.rearrange("(t p) f -> p t f", p=P))
        load_w("q", wq_deq, 0)
        load_w("q", wq_deq, 1)
        load_x(1, 0, 4)
        nc.sync.dma_start(out=mask_rows[:], in_=attention_mask[0].rearrange("(t p) k -> p t k", p=P))
        for b in range(2, B):
            load_x(b, 0, 4)
        cos_by_code = cos_rows[:].rearrange("p s (f q) -> p s q f", q=PACK)
        sin_by_code = sin_rows[:].rearrange("p s (f q) -> p s q f", q=PACK)
        sin_wide = keep.tile([P, TILES, PACK * CHUNKS, 2, HALF_RUN], BF16)
        def tables(t0=0, t1=TILES):
            for table, rows, part, sign in (
                (cos_table, cos_by_code, slice(0, RUN), 1.0),
                (sin_table, sin_by_code, slice(0, HALF_RUN), -1.0),
                (sin_table, sin_by_code, slice(HALF_RUN, RUN), 1.0),
            ):
                nc.scalar.mul(out=table[:, t0:t1, :, part], in_=rows[:, t0:t1, :, part], mul=sign)
        def widen(t):
            nc.scalar.copy(out=sin_wide[:, t].rearrange("p (q c) h f -> p q c (h f)", c=CHUNKS), in_=sin_table[:, t].unsqueeze(2).to_broadcast([P, PACK, CHUNKS, RUN]))

        idle = keep.tile([P, P], BF16)
        if K["DH"] or K["DS"]: nc.vector.memset(idle[:], 0.0)
        def dummy():
            d = psum.tile([P, S], F32, name="dummy", tag="turned", bufs=2)
            nc.tensor.matmul(out=d[:, 0:P], lhsT=idle[:], rhs=idle[:], start=True, stop=True)

        def turn_two_tiles(words, grouped_words, copy_out, tag="misc"):
            bank = psum.tile([P, 2, 2, P], F32, name="bank", tag=tag, bufs=4 if tag == "raw" else 2)
            for r in range(2):
                for u in range(2):
                    nc.tensor.transpose(bank[:, r, u, :], words[:, r, u : 2 * P : 2] if words.ndim == 3 else words[:, r, u, :], ident[:])
            copy_out(out=grouped_words.rearrange("p (r n) u -> p r n u", r=2), in_=bank[:].rearrange("p r u n -> p r n u"))

        def new_mx(pool, tag):
            return (pool.tile([P, 512], U32, name=tag + "_codes", tag=tag + "_codes", align_bytes=K["AL"]), pool.tile([P, 512], U8, name=tag + "_scales", tag=tag + "_scales", align_bytes=K["AL"]))

        def quantise(mx, grouped, lo, hi):
            nc.vector.quantize_mx(out=mx[0][:, lo:hi].bitcast(FP8X4), scales=mx[1][:, lo:hi], in_=grouped[:, lo:hi].rearrange("p n t -> p (n t)"))

        def mx_pass(acc, st, c0, mov, m0):
            cols, mc = slice(c0, c0 + P), slice(m0, m0 + 512)
            nc.tensor.matmul_mx(out=acc, lhsT=st[0][:, cols].bitcast(FP8X4), lhsT_scale=st[1][:, cols], rhs=mov[0][:, mc].bitcast(FP8X4), rhs_scale=mov[1][:, mc], start=True, stop=True)

        w_mx, x_g, x_mx, raw, rot_g, rot_mx, prod = {}, {}, {}, {}, {}, {}, {}

        xp = {}
        def permute_x(b, h):
            xp[b, h] = stage.tile([P, 2, 2, P], F32, name="xp", tag="xp")
            nc.scalar.copy(out=xp[b, h][:], in_=x_rows[b][:].bitcast(F32)[:, 2*h:2*h+2, :].rearrange("p r (n u) -> p r u n", u=2))
        kx_g, kx_mx = {}, {}
        X_COL = (0, 768)
        def stage_kx(b):
            kx_g[b] = stage.tile([P, 1024, PACK], BF16, name="kx_g", tag="kx_g", align_bytes=K["AL"])
            kx_mx[b] = (stage.tile([P, 1024], U32, name="kx_codes", tag="kx_codes", bufs=3, align_bytes=K["AL"]), stage.tile([P, 1024], U8, name="kx_scales", tag="kx_scales", bufs=3, align_bytes=K["AL"]))
        def turn_x(b, h, eng=None):
            if h == 0:
                stage_kx(b - 1)
            f = 2 * h
            turn_two_tiles(xp[b, h][:] if (b, h) in xp else x_rows[b][:].bitcast(F32)[:, f : f + 2, :], kx_g[b - 1][:].rearrange("p n t -> p (n t)").bitcast(F32).rearrange("p (n u) -> p n u", u=2)[:, X_COL[h] : X_COL[h] + 256, :], eng or nc.scalar.copy)
        def quant_x(b, h):
            quantise(kx_mx[b - 1], kx_g[b - 1], X_COL[h], X_COL[h] + 256)

        def jobs(s):
            b, r = divmod(s, 4)
            n = "kkqq"[r]
            return [(n, b, 2 * (r % 2)), (n, b, 2 * (r % 2) + 1)]
        def gparts(s, k):
            if is_w(s, k): return []
            if K["EE"] and s < K["EE"]: return ["low"]
            if K["GP"] == "low2": return ["low"] if k == 1 else []
            if K["GP"] == "mix": return [] if k == 0 else (["low", "high"] if s % 4 in K["GX"] else ["low"])
            if K["GP"] == "low1": return ["low"] if k == 0 else []
            if K["GP"] == "both1odd": return ["low", "high"] if k == 0 and s % 2 else []
            if K["GP"] == "both2even": return ["low", "high"] if k == 1 and s % 2 == 0 else []
            if K["GP"] == "none": return []
            if K["GP"] == "low12": return ["low"]
            if K["GP"] == "both2odd": return ["low", "high"] if k == 1 and s % 2 else []
            if K["GP"] == "lowodd": return ["low"] if k == 1 and s % 2 else []
        def is_w(s, k):
            if K["WE"] and k == 0 and K["WE0"] <= s < K["WE"]: return True
            return K["WJ"] and k == 0 and s % K["WJ"] in K["WP"] and 0 < s < PAIRS - 2
        sums = {}
        PART = dict(low=slice(0, HALF_RUN), high=slice(HALF_RUN, RUN))
        OTHER = dict(low="high", high="low")

        def project(s):
            for j in jobs(s):
                raw[j] = psum.tile([P, H], F32, name="raw", tag="raw", bufs=4)
                mx_pass(raw[j][:], kx_mx[j[1] - 1], X_COL[j[2] // 2] + j[2] % 2 * P, w_mx[j[0]], 0)
        def view(ap): return ap.rearrange("p (q c f) -> p q c f", q=PACK, c=CHUNKS)
        def factor(table, t, part):
            f = table[:, t, :, part]
            return f.unsqueeze(2).to_broadcast([P, PACK, CHUNKS, f.shape[2]])
        tmps = {}
        def g_late(s, tok=False):
            for k, j in enumerate(jobs(s)):
                for n, part in enumerate(gparts(s, k)):
                    if tok and n == 0: nc.vector.memset(prod[j][1][:, 0, 0, 0:1] if part == "low" else prod[j][1][:, 0, 0, HALF_RUN : HALF_RUN + 1], 0.0)
                    nc.gpsimd.tensor_tensor(out=prod[j][1][:][:, :, :, PART[part]], in0=tmps[j, part][:], in1=factor(sin_table, j[2], PART[part]), op=MULT)
        def g_side(s, late=False):
            for k, j in enumerate(jobs(s)):
                prod[j] = (products.tile([P, PACK, CHUNKS, RUN], F32, name="straight", tag="straight"), products.tile([P, PACK, CHUNKS, RUN], F32, name="crossed", tag="crossed"))
                for part in gparts(s, k):
                    tmp = results.tile([P, PACK, CHUNKS, HALF_RUN], F32, name="tmp", tag="tmp")
                    nc.scalar.copy(out=tmp[:], in_=view(raw[j][:])[:, :, :, PART[OTHER[part]]])
                    tmps[j, part] = tmp
                    if late: continue
                    es = K["ESPLIT"]
                    for h in range(es):
                        hs = slice(h * PACK // es, (h + 1) * PACK // es)
                        nc.gpsimd.tensor_tensor(out=prod[j][1][:][:, hs, :, PART[part]], in0=tmp[:, hs], in1=factor(sin_table, j[2], PART[part])[:, hs], op=MULT)
        def v_side(s, k, between=None):
            j = jobs(s)[k]
            nc.vector.tensor_tensor(out=prod[j][0][:], in0=view(raw[j][:]), in1=factor(cos_table, j[2], slice(0, RUN)), op=MULT)
            if between: between()
            if K["SIN1"] and not gparts(s, k) and s >= 2:
                swapped = raw[j][:].rearrange("p (q c h f) -> p q c h f", q=PACK, c=CHUNKS, h=2)[:, :, :, ::-1, :].rearrange("p q c h f -> p (q c) h f")
                nc.vector.tensor_tensor(out=prod[j][1][:].rearrange("p q c (h f) -> p (q c) h f", h=2), in0=swapped, in1=sin_wide[:, j[2]], op=MULT)
                return w_add(s, k, False)
            for part in ("low", "high"):
                if part not in gparts(s, k):
                    nc.vector.tensor_tensor(out=prod[j][1][:, :, :, PART[part]], in0=view(raw[j][:])[:, :, :, PART[OTHER[part]]], in1=factor(sin_table, j[2], PART[part]), op=MULT)
            w_add(s, k, False)
        def w_add(s, k, late):
            j = jobs(s)[k]
            if is_w(s, k):
                if K["WADD"] == "V" and not late: return
                sums[j] = products.tile([P, 2, CHUNKS * RUN, 2], BF16, name="sums", tag="sums")
                a, c = [x[:].rearrange("p (u e) c f -> p u (c f) e", u=2) for x in prod[j]]
                sm = 1 if late else min(2, K["SPLITMASK"])
                for h in range(sm):
                    hs = slice(h * 2 // sm, (h + 1) * 2 // sm)
                    (nc.vector if late else nc.gpsimd).tensor_tensor(out=sums[j][:, hs], in0=a[:, hs], in1=c[:, hs], op=ADD)
        turned = {}
        def t_side(s, k):
            n, b, t = j = jobs(s)[k]
            tn = psum.tile([P, PACK, P], F32, name="turned", tag="turned", bufs=2)
            if is_w(s, k):
                for u in range(2):
                    nc.tensor.transpose(tn[:, u, :], sums[j][:].rearrange("p u n e -> p (u n e)").bitcast(F32)[:, u * P : u * P + P], ident[:])
                turned[j] = tn
                return
            if K["TG"]:
                for i in (0, 1):
                    for c in range(PACK):
                        nc.tensor.matmul(out=tn[:, c, :], lhsT=prod[j][i][:, c].rearrange("p c f -> p (c f)"), rhs=ident[:], is_transpose=True, start=i == 0 and c == 0, stop=i == 1 and c == PACK - 1)
                turned[j] = tn
                return
            for c in range(PACK):
                for i in (0, 1):
                    nc.tensor.matmul(out=tn[:, c, :], lhsT=prod[j][i][:, c].rearrange("p c f -> p (c f)"), rhs=ident[:], is_transpose=True, start=i == 0, stop=i == 1)
            turned[j] = tn
        def t_both(s):
            js = jobs(s)
            for j in js: turned[j] = psum.tile([P, PACK, P], F32, name="turned", tag="turned", bufs=2)
            for c in range(PACK):
                for i in (0, 1):
                    for j in js:
                        nc.tensor.matmul(out=turned[j][:, c, :], lhsT=prod[j][i][:, c].rearrange("p c f -> p (c f)"), rhs=ident[:], is_transpose=True, start=i == 0, stop=i == 1)
        def s_side(s, k, eng=None):
            n, b, t = j = jobs(s)[k]
            if (n, b) not in rot_g:
                if n == "q":
                    rot_g[n, b] = stage.tile([P, S, PACK], BF16, name=n + "_rot", tag=n + "_rot", align_bytes=K["AL"])
                    rot_mx[n, b] = new_mx(stage, n + "rot")
                else:
                    if b not in kx_g: stage_kx(b)
                    rot_g[n, b] = kx_g[b][:, 256:768]
            if is_w(s, k):
                (eng or nc.scalar.copy)(out=rot_g[n, b][:, :, :].rearrange("p n t -> p (n t)").bitcast(F32).rearrange("p (n u) -> p n u", u=2)[:, t * P : (t + 1) * P, :], in_=turned[j][:, 0:2].rearrange("p c n -> p n c"))
                return
            (eng or nc.scalar.copy)(out=rot_g[n, b][:, t * P : (t + 1) * P, :], in_=turned[j][:].rearrange("p c n -> p n c"))
        def quant_rot(s):
            n, b, t = jobs(s)[0]
            if n == "q":
                quantise(rot_mx[n, b], rot_g[n, b], t * P, t * P + 256)
            else:
                lo, hi = (0, 512) if t == 0 else (512, 1024)
                if b == B - 1: lo, hi = max(lo, 256), min(hi, 768)
                quantise(kx_mx[b], kx_g[b], lo, hi)
        def score(b, t):
            sc = psum.tile([P, S], F32, name="scores", tag="misc", bufs=2)
            mx_pass(sc[:], rot_mx["q", b], t * P, kx_mx[b], 256)
            return sc
        def scale(b, t, sc):
            res = results.tile([P, S], F32, name="res", tag="res")
            nc.scalar.mul(out=res[:], in_=sc[:], mul=INV_SQRT_HD)
            return b, t, res
        def add_mask(b, t, res):
            nc.gpsimd.tensor_tensor(out=res[:], in0=res[:], in1=mask_rows[:, t, :], op=ADD)
            nc.sync.dma_start(out=out[b, t * P : (t + 1) * P, :], in_=res[:])
        def finish(b, t, sc, onv=False):
            res = results.tile([P, S], F32, name="res", tag="res")
            if onv:
                nc.vector.scalar_tensor_tensor(out=res[:], in0=sc[:], scalar=INV_SQRT_HD, in1=mask_rows[:, t, :], op0=MULT, op1=ADD)
            elif K["ACC"]:
                nc.scalar.mul(out=res[:], in_=sc[:], mul=INV_SQRT_HD)
                nc.sync.dma_start(out=out[b, t * P : (t + 1) * P, :], in_=res[:])
                if t == 3: nc.gpsimd.dma_start(out=out[b].rearrange("(t p) k -> p t k", p=P), in_=mask_f32[:], accum_op=ADD)
                return
            else:
                nc.scalar.mul(out=res[:], in_=sc[:], mul=INV_SQRT_HD)
                w = S // K["SPLITMASK"]
                for h in range(K["SPLITMASK"]):
                    nc.gpsimd.tensor_tensor(out=res[:, h*w:h*w+w], in0=res[:, h*w:h*w+w], in1=mask_rows[:, t, h*w:h*w+w], op=ADD)
            nc.sync.dma_start(out=out[b, t * P : (t + 1) * P, :], in_=res[:])

        wg = {}
        def turn_w(n, h, eng):
            if h == 0:
                wg[n] = keep.tile([P, H, PACK], BF16, name=n + "_w_g", tag=n + "_w_g", align_bytes=K["AL"])
                w_mx[n] = new_mx(keep, n + "_w")
            f = 2 * h
            turn_two_tiles(w_rows[n][:].bitcast(F32)[:, f : f + 2, :], wg[n][:].rearrange("p n t -> p (n t)").bitcast(F32).rearrange("p (n u) -> p n u", u=2)[:, f * P : (f + 2) * P, :], eng, tag="raw")
        def quant_w(n, h): quantise(w_mx[n], wg[n], 256 * h, 256 * h + 256)
        for i in range(K["DH"]): dummy()
        if K["HEAD"]:
            turn_w("k", 0, nc.vector.tensor_copy)
            turn_w("k", 1, nc.scalar.copy)
            turn_x(0, 0)
            turn_x(0, 1)
            quant_w("k", 0)
            quant_w("k", 1)
            quant_x(0, 0)
            tables(0, 2)
            for i in range(K["DM"]): dummy()
            project(0)
            tables(2, 4)
        else:
            turn_w("k", 0, nc.vector.tensor_copy)
            turn_w("k", 1, nc.scalar.copy)
            turn_x(0, 0, nc.vector.tensor_copy)
            turn_x(0, 1)
            quant_w("k", 0)
            quant_w("k", 1)
            quant_x(0, 0)
            tables()
            for i in range(K["DM"]): dummy()
            project(0)
        turn_w("q", 0, nc.scalar.copy)
        turn_w("q", 1, nc.scalar.copy)
        g_side(0)
        if K["ACC"]:
            mask_f32 = keep.tile([P, TILES, S], F32)
            nc.gpsimd.tensor_copy(out=mask_f32[:], in_=mask_rows[:])
        sched = {}
        for b in range(B):
            for t in range(TILES):
                st = 4 * b + K["LAGS"][t]
                if b == B - 1: st = 99
                if st == 32: st = 31
                sched.setdefault(st, []).append((b, t))
        for s in range(PAIRS):
            b, r = divmod(s, 4)
            if s == 0:
                v_side(s, 0)
                quant_x(0, 1)
            if K["SF"]:
                scs = [(bb, tt, score(bb, tt)) for bb, tt in sched.get(s, [])]
            if s + 1 < PAIRS:
                project(s + 1)
            ql = 2 if K["QPOS"] == 2 else 1
            def quants():
                if s >= ql: quant_rot(s - ql)
            if 0 < s < PAIRS: v_side(s, 0, quants if K["QPOS"] == 2 else None)
            if K["QPOS"] == 0: quants()
            if s < K["DS"]: dummy()
            if not K["SF"] and not K["SMID"]: scs = [(bb, tt, score(bb, tt)) for bb, tt in sched.get(s, [])]
            if K["SMID"]: scs = []
            if K["TOK"]:
                if s + 1 < PAIRS: g_side(s + 1, True)
                held = [scale(*x) for x in scs]
                scs = []
            elif s + 1 < PAIRS and not K["MF"]: g_side(s + 1)
            for idx, (bb, tt, sc) in enumerate(scs): finish(bb, tt, sc, onv=K["MASKV"] and tt == 3 and bb % K["MASKV"] == 0)
            if s + 1 < PAIRS and K["MF"]: g_side(s + 1)
            if K["XP"] and r in (2, 3) and b + 2 < B: permute_x(b + 2, r - 2)
            xr = (0, 1)
            if r in xr and b + 1 < B: turn_x(b + 1, r - xr[0])
            if s < PAIRS:
                if not is_w(s, 0) and not K["TI"]:
                    t_side(s, 0)
                    s_side(s, 0)
                if K["SMID"]:
                    for bb, tt in sched.get(s, []): finish(bb, tt, score(bb, tt))
                v_side(s, 1)
                if K["WADD"] == "V" and not K["WQ"]: w_add(s, 0, True)
                if s == 0:
                    quant_w("q", 0)
                    quant_w("q", 1)
                if K["QPOS"] == 1: quants()
                if K["WADD"] == "V" and K["WQ"]: w_add(s, 0, True)
                if K["TOK"]:
                    if K["TOK"] == 2 and held:
                        add_mask(*held[0])
                        held = held[1:]
                    if s + 1 < PAIRS: g_late(s + 1, K["TOK"] != 3)
                    for x in held: add_mask(*x)
                if K["TI"]:
                    t_both(s)
                    s_side(s, 0)
                else: t_side(s, 1)
                s_side(s, 1)
                if K["SIN1"] and s < 2: widen(2 * s)
                if is_w(s, 0):
                    t_side(s, 0)
                    s_side(s, 0)
        if K["QPOS"] == 2: quant_rot(PAIRS - 2)
        b = B - 1
        late = [(b - 1, t) for t in range(TILES) if 4 * (b - 1) + K["LAGS"][t] >= PAIRS and 4 * (b - 1) + K["LAGS"][t] != 32]
        if K["TAIL"]:
            for bb, t in late: finish(bb, t, score(bb, t))
            if K["TAIL"] == 2:
                ss = [score(b, 0), score(b, 1)]
                finish(b, 0, ss[0])
                quantise(rot_mx["q", b], rot_g["q", b], 2 * P, 3 * P)
                finish(b, 1, ss[1], onv=True)
                quantise(rot_mx["q", b], rot_g["q", b], 3 * P, 4 * P)
            else:
                finish(b, 0, score(b, 0))
                finish(b, 1, score(b, 1), onv=True)
                quant_rot(PAIRS - 1)
            for t in (2, 3): finish(b, t, score(b, t), onv=True)
        else:
            for bb, t in late + [(b, 0), (b, 1)]:
                finish(bb, t, score(bb, t))
            quant_rot(PAIRS - 1)
            for t in (2, 3):
                finish(b, t, score(b, t), onv=not K["ACC"])
